import numpy as np
import ml_dtypes


def mxq(x, axis, fmt="e4m3"):
    dtype, down = {"e4m3": (ml_dtypes.float8_e4m3fn, 7), "e5m2": (ml_dtypes.float8_e5m2, 14)}[fmt]
    v = np.moveaxis(np.asarray(x, np.float32).astype(ml_dtypes.bfloat16).astype(np.float64), axis, -1)
    blocks = v.reshape(v.shape[:-1] + (-1, 32))
    amax = np.abs(blocks).max(-1, keepdims=True)
    byte = np.maximum(np.where(amax > 0, np.frexp(amax)[1] - 1 + 127, 0) - down, 1)
    scale = np.exp2(byte - 127.0)
    codes = (blocks / scale).astype(np.float32).astype(dtype).astype(np.float64)
    return np.moveaxis((codes * scale).reshape(v.shape), -1, axis)


WIDE = False


def mx_kscale(k):
    if not WIDE:
        return np.ones(k)
    levels = np.array([10, -10, 5, -5, 0])
    a = np.random.permutation(np.resize(levels, k // 512 * 4)).reshape(k // 512, 4)
    idx = np.arange(k)
    return np.exp2(a[idx // 512, idx % 128 // 32])


BF16 = ml_dtypes.bfloat16


def bf(x):
    return np.asarray(x, np.float32).astype(BF16)


def f64(x):
    return np.asarray(x).astype(np.float64)


B, C, O, M, K, NR, NT = 2, 512, 256, 4, 32, 8, 8
BN_EPS = 1e-5


def setup_inputs():
    s = mx_kscale(C)

    def p(gain):
        return bf(np.random.standard_normal((O, C)) * gain / np.sqrt(C) / s[None, :])

    return {"A": bf(np.random.standard_normal((B, C, M, K, NR, NT)) * s[None, :, None, None, None, None]),
            "P1": p(1.0), "P2": p(2.0 * np.sqrt(M)), "P3": p(2.0 * np.sqrt(NT)), "P4": p(np.sqrt(NR)),
            "a5": bf(np.random.standard_normal((B, O, M, K, NT)) * 1.2 / np.sqrt(K)),
            "gamma": bf(1.0 + 0.2 * np.random.standard_normal(O)),
            "beta": bf(0.3 * np.random.standard_normal(O))}


def mix(P, X):
    y = mxq(f64(P), 1, "e4m3") @ mxq(X.reshape(B, C, -1), 1, "e4m3")
    return y.reshape((B, O) + X.shape[2:])


def reference(A, P1, P2, P3, P4, a5, gamma, beta):
    Af = f64(A)
    A1 = mix(P1, Af)
    A2 = mix(P2, Af.mean(2))[:, :, None]
    A3 = mix(P3, Af.mean(5))[..., None]
    A4 = mix(P4, Af.mean(4))[:, :, :, :, None, :]
    A5 = f64(a5)[:, :, :, :, None, :]
    y = A1 + 0.1 * A2 + 0.1 * A3 + 0.5 * A4 + 2.0 * A5
    y = np.maximum(y, 0.0)
    ax = (0, 2, 3, 4, 5)
    mean = y.mean(axis=ax, keepdims=True)
    var = y.var(axis=ax, keepdims=True)
    g = f64(gamma)[None, :, None, None, None, None]
    bta = f64(beta)[None, :, None, None, None, None]
    return (y - mean) * (1.0 / np.sqrt(var + BN_EPS)) * g + bta

@@ -1,0 +1,315 @@
+from contextlib import ExitStack
+
+import concourse.mybir as mybir
+from concourse.masks import make_identity
+
+BF16 = mybir.dt.bfloat16
+F32 = mybir.dt.float32
+I32 = mybir.dt.int32
+U32 = mybir.dt.uint32
+U8 = mybir.dt.uint8
+FP8X4 = mybir.dt.float8_e4m3fn_x4
+ALU = mybir.AluOpType
+ACT = mybir.ActivationFunctionType
+AXIS_X = mybir.AxisListType.X
+
+B, C, O, M, K, NR, NT = 2, 512, 256, 4, 32, 8, 8
+BN_EPS = 1e-5
+P = 128
+PACK = 4
+O_TILES = O // P
+POSITIONS = M * K * NR * NT
+
+K_PIECE = 4
+PIECES_PER_B = K // K_PIECE
+N_PIECES = B * PIECES_PER_B
+KR = K_PIECE * NR
+RUN = K_PIECE * NR * NT
+COLS = M * RUN
+SMALL = M * KR
+
+UP = 10.0
+STATIONARY = (("p1", 8.0), ("p1", 2.0), ("p2", 1.0), ("p3", 1.0), ("p4", 4.0), ("p4", 1.0))
+W_A1_HI, W_A1_LO, W_A2, W_A3, W_A4_HI, W_A4_LO = 0, 1, 2, 3, 4, 5
+
+STORE_COLS = 2048
+
+FLOPS = 2 * O * C * B * POSITIONS * (8 + 2 + 1 + 1) // 8
+
+
+def tile_layer_3d_dep_pa_t_kernel(tc, A, P1, P2, P3, P4, a5, gamma, beta, out):
+    nc = tc.nc
+    weights = {"p1": P1, "p2": P2, "p3": P3, "p4": P4}
+
+    with ExitStack() as ctx:
+        keep = ctx.enter_context(tc.tile_pool(name="keep", bufs=1))
+        psum_x = ctx.enter_context(tc.psum_pool(name="psum_x", bufs=4))
+        psum_small = ctx.enter_context(tc.psum_pool(name="psum_small", bufs=2))
+
+        w_codes = keep.tile([P, len(STATIONARY), O], U32, align_bytes=64)
+        w_scales = keep.tile([P, len(STATIONARY), O], U8, align_bytes=64)
+        a5_sb = keep.tile([P, B * O_TILES, M * K * NT], BF16)
+        gamma_beta = keep.tile([P, 2 * O_TILES], F32)
+        y = keep.tile([P, O_TILES, B, POSITIONS], F32)
+        sums = keep.tile([P, O_TILES, N_PIECES], F32)
+        squares = keep.tile([P, O_TILES, N_PIECES], F32)
+        at_scales = keep.tile([P, SMALL], U8, align_bytes=64)
+        nc.vector.memset(at_scales[:].bitcast(I32), 0)
+
+        nc.sync.dma_start(
+            out=a5_sb[:], in_=a5.rearrange("b (ot o) m k t -> o (b ot) (m k t)", o=P)
+        )
+
+        with tc.tile_pool(name="setup", bufs=2) as setup:
+            ident_f32 = setup.tile([P, P], F32, tag="ident_f32")
+            make_identity(nc, ident_f32[:])
+            ident_bf16 = setup.tile([P, P], BF16, tag="ident_bf16")
+            make_identity(nc, ident_bf16[:])
+
+            grouped_w = {}
+            for name in ("p1", "p2", "p3", "p4"):
+                w_rows = setup.tile([P, O_TILES, C], BF16, tag="w_rows")
+                nc.sync.dma_start(
+                    out=w_rows[:], in_=weights[name].rearrange("(ot o) c -> o ot c", o=P)
+                )
+                words = w_rows[:].bitcast(F32).rearrange("o ot (p u) -> o ot u p", u=2)
+                turned = psum_small.tile([P, O_TILES, 2, P], F32, tag="small")
+                for ot in range(O_TILES):
+                    for u in range(2):
+                        nc.tensor.transpose(turned[:, ot, u, :], words[:, ot, u, :], ident_f32[:])
+                grouped = setup.tile([P, O * PACK], BF16, name="grouped_" + name, bufs=1)
+                nc.vector.tensor_copy(
+                    out=grouped[:].bitcast(F32).rearrange("p (ot o u) -> p ot o u", ot=O_TILES, u=2),
+                    in_=turned[:].rearrange("p ot u o -> p ot o u"),
+                )
+                grouped_w[name] = grouped
+
+            for i, (name, factor) in enumerate(STATIONARY):
+                scaled = setup.tile([P, O * PACK], BF16, tag="scaled", align_bytes=64)
+                nc.vector.tensor_scalar_mul(out=scaled[:], in0=grouped_w[name][:], scalar1=factor)
+                nc.vector.quantize_mx(
+                    out=w_codes[:, i, :].bitcast(FP8X4), scales=w_scales[:, i, :], in_=scaled[:]
+                )
+
+            gb_rows = setup.tile([P, P], BF16, tag="gb_rows")
+            nc.vector.memset(gb_rows[:], 0.0)
+            nc.sync.dma_start(out=gb_rows[0:O_TILES, :], in_=gamma.rearrange("(ot o) -> ot o", o=P))
+            nc.sync.dma_start(
+                out=gb_rows[O_TILES : 2 * O_TILES, :], in_=beta.rearrange("(ot o) -> ot o", o=P)
+            )
+            gb_turned = psum_small.tile([P, P], BF16, tag="small")
+            nc.tensor.transpose(gb_turned[:], gb_rows[:], ident_bf16[:])
+            nc.vector.tensor_copy(out=gamma_beta[:], in_=gb_turned[:, 0 : 2 * O_TILES])
+
+        stream = ctx.enter_context(tc.tile_pool(name="stream", bufs=2))
+        single = ctx.enter_context(tc.tile_pool(name="single", bufs=1))
+
+        def mix(acc, weight, ot, codes, scales, start, stop):
+            nc.tensor.matmul_mx(
+                out=acc,
+                lhsT=w_codes[:, weight, ot * P : (ot + 1) * P].bitcast(FP8X4),
+                lhsT_scale=w_scales[:, weight, ot * P : (ot + 1) * P],
+                rhs=codes.bitcast(FP8X4),
+                rhs_scale=scales,
+                start=start,
+                stop=stop,
+            )
+
+        for piece in range(N_PIECES):
+            b, kq = divmod(piece, PIECES_PER_B)
+
+            raw = stream.tile([P, PACK, M, RUN], BF16)
+            nc.sync.dma_start(
+                out=raw[:],
+                in_=A[b].rearrange("(p j) m k r t -> p j m (k r t)", j=PACK)[
+                    :, :, :, kq * RUN : (kq + 1) * RUN
+                ],
+            )
+
+            grouped_a = stream.tile([P, COLS, PACK], BF16, align_bytes=64)
+            for m in range(M):
+                nc.vector.tensor_copy(
+                    out=grouped_a[:, m * RUN : (m + 1) * RUN, :].rearrange(
+                        "p (t x) j -> p t x j", t=NT
+                    ),
+                    in_=raw[:, :, m, :].rearrange("p j (x t) -> p t x j", t=NT),
+                )
+            a_codes = stream.tile([P, COLS], U32, align_bytes=64)
+            a_scales = stream.tile([P, COLS], U8, align_bytes=64)
+            nc.vector.quantize_mx(
+                out=a_codes[:].bitcast(FP8X4),
+                scales=a_scales[:],
+                in_=grouped_a[:].rearrange("p w j -> p (w j)"),
+            )
+
+            pair_sums = single.tile([P, PACK, 2, RUN], F32)
+            nc.vector.tensor_add(out=pair_sums[:], in0=raw[:, :, 0:2, :], in1=raw[:, :, 2:4, :])
+            m_sums = single.tile([P, PACK, RUN], F32)
+            nc.vector.tensor_add(out=m_sums[:], in0=pair_sums[:, :, 0, :], in1=pair_sums[:, :, 1, :])
+            grouped_am = stream.tile([P, RUN, PACK], BF16, align_bytes=64)
+            nc.scalar.activation(
+                out=grouped_am[:].rearrange("p (t x) j -> p t x j", t=NT),
+                in_=m_sums[:].rearrange("p j (x t) -> p t x j", t=NT),
+                func=ACT.Copy,
+                scale=1.0 / M,
+            )
+            am_codes = stream.tile([P, RUN], U32, align_bytes=64)
+            am_scales = stream.tile([P, RUN], U8, align_bytes=64)
+            nc.vector.quantize_mx(
+                out=am_codes[:].bitcast(FP8X4),
+                scales=am_scales[:],
+                in_=grouped_am[:].rearrange("p w j -> p (w j)"),
+            )
+
+            t_sums = single.tile([P, PACK, SMALL], F32)
+            nc.vector.tensor_reduce(
+                out=t_sums[:].rearrange("p j x -> p (j x)"),
+                in_=raw[:].rearrange("p j m (x t) -> p (j m x) t", t=NT),
+                axis=AXIS_X,
+                op=ALU.add,
+            )
+            grouped_at = stream.tile([P, SMALL, PACK], BF16, align_bytes=64)
+            nc.scalar.activation(
+                out=grouped_at[:],
+                in_=t_sums[:].rearrange("p j x -> p x j"),
+                func=ACT.Copy,
+                scale=1.0 / NT,
+            )
+            at_codes = stream.tile([P, SMALL], U32, align_bytes=64)
+            nc.vector.quantize_mx(
+                out=at_codes[:].bitcast(FP8X4),
+                scales=at_scales[:],
+                in_=grouped_at[:].rearrange("p w j -> p (w j)"),
+            )
+            at_rep_codes = stream.tile([P, COLS], U32, align_bytes=64)
+            at_rep_scales = stream.tile([P, COLS], U8, align_bytes=64)
+            nc.vector.tensor_copy(
+                out=at_rep_codes[:].bitcast(I32).rearrange("p (m t x) -> p m t x", m=M, t=NT),
+                in_=at_codes[:]
+                .bitcast(I32)
+                .rearrange("p (m x) -> p m x", m=M)
+                .unsqueeze(2)
+                .to_broadcast([P, M, NT, KR]),
+            )
+            nc.vector.tensor_copy(
+                out=at_rep_scales[:].bitcast(I32).rearrange("p (m t x) -> p m t x", m=M, t=NT),
+                in_=at_scales[:]
+                .bitcast(I32)
+                .rearrange("p (m x) -> p m x", m=M)
+                .unsqueeze(2)
+                .to_broadcast([P, M, NT, KR // 4]),
+            )
+
+            r_sums = single.tile([P, PACK, SMALL], F32)
+            nc.vector.tensor_reduce(
+                out=r_sums[:].rearrange("p j (x t) -> p (j x) t", t=NT),
+                in_=raw[:].rearrange("p j m (k r t) -> p (j m k) t r", r=NR, t=NT),
+                axis=AXIS_X,
+                op=ALU.add,
+            )
+            grouped_ar = stream.tile([P, SMALL, PACK], BF16, align_bytes=64)
+            nc.scalar.activation(
+                out=grouped_ar[:],
+                in_=r_sums[:].rearrange("p j x -> p x j"),
+                func=ACT.Copy,
+                scale=1.0 / NR,
+            )
+            ar_codes = stream.tile([P, SMALL], U32, align_bytes=64)
+            ar_scales = stream.tile([P, SMALL], U8, align_bytes=64)
+            nc.vector.quantize_mx(
+                out=ar_codes[:].bitcast(FP8X4),
+                scales=ar_scales[:],
+                in_=grouped_ar[:].rearrange("p w j -> p (w j)"),
+            )
+
+            for ot in range(O_TILES):
+                a4_acc = psum_small.tile([P, SMALL], F32, tag="small")
+                mix(a4_acc[:], W_A4_HI, ot, ar_codes[:], ar_scales[:], True, False)
+                mix(a4_acc[:], W_A4_LO, ot, ar_codes[:], ar_scales[:], False, True)
+                no_r = stream.tile([P, M, K_PIECE, NT], F32)
+                nc.vector.scalar_tensor_tensor(
+                    out=no_r[:].rearrange("p m k t -> p m (k t)"),
+                    in0=a5_sb[:, b * O_TILES + ot, :].rearrange(
+                        "p (m kq x) -> p m kq x", m=M, kq=PIECES_PER_B
+                    )[:, :, kq, :],
+                    scalar=2.0 * UP,
+                    in1=a4_acc[:].rearrange("p (m x) -> p m x", m=M),
+                    op0=ALU.mult,
+                    op1=ALU.add,
+                )
+
+                y_piece = y[:, ot, b, :].rearrange("p (m kq x) -> p m kq x", m=M, kq=PIECES_PER_B)[
+                    :, :, kq, :
+                ]
+                for m0 in range(0, M, 2):
+                    acc = psum_x.tile([P, 2, RUN], F32)
+                    for i in range(2):
+                        cols = slice((m0 + i) * RUN, (m0 + i + 1) * RUN)
+                        mix(acc[:, i, :], W_A1_HI, ot, a_codes[:, cols], a_scales[:, cols], True, False)
+                        mix(acc[:, i, :], W_A1_LO, ot, a_codes[:, cols], a_scales[:, cols], False, False)
+                        mix(acc[:, i, :], W_A2, ot, am_codes[:], am_scales[:], False, False)
+                        mix(
+                            acc[:, i, :], W_A3, ot, at_rep_codes[:, cols], at_rep_scales[:, cols],
+                            False, True,
+                        )
+                    nc.vector.tensor_tensor(
+                        out=y_piece[:, m0 : m0 + 2, :].rearrange(
+                            "p m (k r t) -> p m k r t", r=NR, t=NT
+                        ),
+                        in0=acc[:].rearrange("p m (t k r) -> p m k r t", t=NT, r=NR),
+                        in1=no_r[:, m0 : m0 + 2, :, :]
+                        .unsqueeze(3)
+                        .to_broadcast([P, 2, K_PIECE, NR, NT]),
+                        op=ALU.add,
+                    )
+
+                nc.scalar.activation(
+                    out=y_piece, in_=y_piece, func=ACT.Relu,
+                    accum_out=sums[:, ot, piece : piece + 1],
+                )
+                squared = stream.tile([P, M, RUN], BF16)
+                nc.scalar.activation(
+                    out=squared[:], in_=y_piece, func=ACT.Square,
+                    accum_out=squares[:, ot, piece : piece + 1],
+                )
+
+        count = float(B * POSITIONS)
+        mean = single.tile([P, O_TILES], F32)
+        nc.vector.tensor_reduce(out=mean[:], in_=sums[:], axis=AXIS_X, op=ALU.add)
+        nc.vector.tensor_scalar_mul(out=mean[:], in0=mean[:], scalar1=1.0 / count)
+        var = single.tile([P, O_TILES], F32)
+        nc.vector.tensor_reduce(out=var[:], in_=squares[:], axis=AXIS_X, op=ALU.add)
+        nc.vector.tensor_scalar_mul(out=var[:], in0=var[:], scalar1=1.0 / count)
+        mean_sq = single.tile([P, O_TILES], F32)
+        nc.vector.tensor_mul(out=mean_sq[:], in0=mean[:], in1=mean[:])
+        nc.vector.tensor_sub(out=var[:], in0=var[:], in1=mean_sq[:])
+        nc.vector.tensor_scalar(
+            out=var[:], in0=var[:], scalar1=0.0, scalar2=BN_EPS * UP * UP, op0=ALU.max, op1=ALU.add
+        )
+        std = single.tile([P, O_TILES], F32)
+        nc.scalar.sqrt(out=std[:], in_=var[:])
+        gain = single.tile([P, O_TILES], F32)
+        nc.vector.reciprocal(out=gain[:], in_=std[:])
+        nc.vector.tensor_mul(out=gain[:], in0=gain[:], in1=gamma_beta[:, 0:O_TILES])
+        shift = single.tile([P, O_TILES], F32)
+        nc.vector.tensor_mul(out=shift[:], in0=mean[:], in1=gain[:])
+        nc.vector.tensor_sub(out=shift[:], in0=gamma_beta[:, O_TILES : 2 * O_TILES], in1=shift[:])
+
+        step = 0
+        for b in range(B):
+            out_b = out[b].rearrange("(ot o) m k r t -> o ot (m k r t)", o=P)
+            for ot in range(O_TILES):
+                for c0 in range(0, POSITIONS, STORE_COLS):
+                    part = y[:, ot, b, c0 : c0 + STORE_COLS]
+                    if step % 2 == 0:
+                        nc.vector.tensor_scalar(
+                            out=part, in0=part, scalar1=gain[:, ot : ot + 1],
+                            scalar2=shift[:, ot : ot + 1], op0=ALU.mult, op1=ALU.add,
+                        )
+                    else:
+                        nc.scalar.activation(
+                            out=part, in_=part, func=ACT.Identity,
+                            bias=shift[:, ot : ot + 1], scale=gain[:, ot : ot + 1],
+                        )
+                    nc.sync.dma_start(out=out_b[:, ot, c0 : c0 + STORE_COLS], in_=part)
+                    step += 1

@@ -27,6 +27,9 @@ KR = K_PIECE * NR
 RUN = K_PIECE * NR * NT
 COLS = M * RUN
 SMALL = M * KR
+HALVES = RUN // P
+K_SQUARE = K_PIECE // HALVES
+POOLED = K_SQUARE * NR
 
 UP = 10.0
 STATIONARY = (("p1", 8.0), ("p1", 2.0), ("p2", 1.0), ("p3", 1.0), ("p4", 4.0), ("p4", 1.0))
@@ -43,8 +46,10 @@ def tile_layer_3d_dep_pa_t_kernel(tc, A, P1, P2, P3, P4, a5, gamma, beta, out):
 
     with ExitStack() as ctx:
         keep = ctx.enter_context(tc.tile_pool(name="keep", bufs=1))
-        psum_x = ctx.enter_context(tc.psum_pool(name="psum_x", bufs=4))
-        psum_small = ctx.enter_context(tc.psum_pool(name="psum_small", bufs=2))
+        psum_x = ctx.enter_context(tc.psum_pool(name="psum_x", bufs=3))
+        psum_turned = ctx.enter_context(tc.psum_pool(name="psum_turned", bufs=2))
+        psum_pooled = ctx.enter_context(tc.psum_pool(name="psum_pooled", bufs=2))
+        psum_small = ctx.enter_context(tc.psum_pool(name="psum_small", bufs=1))
 
         w_codes = keep.tile([P, len(STATIONARY), O], U32, align_bytes=64)
         w_scales = keep.tile([P, len(STATIONARY), O], U8, align_bytes=64)
@@ -53,8 +58,11 @@ def tile_layer_3d_dep_pa_t_kernel(tc, A, P1, P2, P3, P4, a5, gamma, beta, out):
         y = keep.tile([P, O_TILES, B, POSITIONS], F32)
         sums = keep.tile([P, O_TILES, N_PIECES], F32)
         squares = keep.tile([P, O_TILES, N_PIECES], F32)
-        at_scales = keep.tile([P, SMALL], U8, align_bytes=64)
-        nc.vector.memset(at_scales[:].bitcast(I32), 0)
+        tr_scales = keep.tile([P, 2 * SMALL], U8, align_bytes=64)
+        nc.vector.memset(tr_scales[:].bitcast(I32), 0)
+        ident_bf16 = keep.tile([P, P], BF16)
+        make_identity(nc, ident_bf16[:])
+        pool_mat = keep.tile([P, 2, POOLED], BF16)
 
         nc.sync.dma_start(
             out=a5_sb[:], in_=a5.rearrange("b (ot o) m k t -> o (b ot) (m k t)", o=P)
@@ -63,8 +71,22 @@ def tile_layer_3d_dep_pa_t_kernel(tc, A, P1, P2, P3, P4, a5, gamma, beta, out):
         with tc.tile_pool(name="setup", bufs=2) as setup:
             ident_f32 = setup.tile([P, P], F32, tag="ident_f32")
             make_identity(nc, ident_f32[:])
-            ident_bf16 = setup.tile([P, P], BF16, tag="ident_bf16")
-            make_identity(nc, ident_bf16[:])
+
+            pool_ones = setup.tile([P, 2, POOLED], F32, tag="pool_ones")
+            nc.vector.tensor_reduce(
+                out=pool_ones[:, 0, :],
+                in_=ident_f32[:].rearrange("p (x t) -> p x t", t=NT),
+                axis=AXIS_X,
+                op=ALU.add,
+            )
+            nc.vector.tensor_reduce(
+                out=pool_ones[:, 1, :].rearrange("p (k t) -> p k t", t=NT),
+                in_=ident_f32[:].rearrange("p (k r t) -> p k t r", r=NR, t=NT),
+                axis=AXIS_X,
+                op=ALU.add,
+            )
+            nc.vector.tensor_scalar_mul(out=pool_mat[:, 0, :], in0=pool_ones[:, 0, :], scalar1=1.0 / NT)
+            nc.vector.tensor_scalar_mul(out=pool_mat[:, 1, :], in0=pool_ones[:, 1, :], scalar1=1.0 / NR)
 
             grouped_w = {}
             for name in ("p1", "p2", "p3", "p4"):
@@ -103,6 +125,7 @@ def tile_layer_3d_dep_pa_t_kernel(tc, A, P1, P2, P3, P4, a5, gamma, beta, out):
 
         stream = ctx.enter_context(tc.tile_pool(name="stream", bufs=2))
         single = ctx.enter_context(tc.tile_pool(name="single", bufs=1))
+        turned_pool = ctx.enter_context(tc.tile_pool(name="turned_pool", bufs=3))
 
         def mix(acc, weight, ot, codes, scales, start, stop):
             nc.tensor.matmul_mx(
@@ -161,31 +184,47 @@ def tile_layer_3d_dep_pa_t_kernel(tc, A, P1, P2, P3, P4, a5, gamma, beta, out):
                 in_=grouped_am[:].rearrange("p w j -> p (w j)"),
             )
 
-            t_sums = single.tile([P, PACK, SMALL], F32)
-            nc.vector.tensor_reduce(
-                out=t_sums[:].rearrange("p j x -> p (j x)"),
-                in_=raw[:].rearrange("p j m (x t) -> p (j m x) t", t=NT),
-                axis=AXIS_X,
-                op=ALU.add,
-            )
-            grouped_at = stream.tile([P, SMALL, PACK], BF16, align_bytes=64)
-            nc.scalar.activation(
-                out=grouped_at[:],
-                in_=t_sums[:].rearrange("p j x -> p x j"),
-                func=ACT.Copy,
-                scale=1.0 / NT,
-            )
-            at_codes = stream.tile([P, SMALL], U32, align_bytes=64)
+            pooled = [
+                psum_pooled.tile([P, 2, PACK, 2, HALVES, POOLED], F32, name="pooled%d" % i, tag="pooled")
+                for i in range(M // 2)
+            ]
+            for j in range(PACK):
+                turned_ps = psum_turned.tile([P, M, HALVES, P], BF16)
+                for m in range(M):
+                    for h in range(HALVES):
+                        nc.tensor.transpose(
+                            turned_ps[:, m, h, :], raw[:, j, m, h * P : (h + 1) * P], ident_bf16[:]
+                        )
+                turned = turned_pool.tile([P, M, HALVES, P], BF16)
+                nc.scalar.copy(out=turned[:], in_=turned_ps[:])
+                for m in range(M):
+                    for h in range(HALVES):
+                        nc.tensor.matmul(
+                            out=pooled[m // 2][:, :, j, m % 2, h, :],
+                            lhsT=turned[:, m, h, :],
+                            rhs=pool_mat[:],
+                            start=True,
+                            stop=True,
+                        )
+            grouped_tr = stream.tile([P, 2, SMALL, PACK], BF16, align_bytes=64)
+            for i in range(M // 2):
+                nc.scalar.copy(
+                    out=grouped_tr[:, :, i * (SMALL // 2) : (i + 1) * (SMALL // 2), :],
+                    in_=pooled[i][:].rearrange("p s j m h x -> p s (m h x) j"),
+                )
+            tr_codes = stream.tile([P, 2 * SMALL], U32, align_bytes=64)
             nc.vector.quantize_mx(
-                out=at_codes[:].bitcast(FP8X4),
-                scales=at_scales[:],
-                in_=grouped_at[:].rearrange("p w j -> p (w j)"),
+                out=tr_codes[:].bitcast(FP8X4),
+                scales=tr_scales[:],
+                in_=grouped_tr[:].rearrange("p s w j -> p (s w j)"),
             )
+            at_codes, at_scales = tr_codes[:, 0:SMALL], tr_scales[:, 0:SMALL]
+            ar_codes, ar_scales = tr_codes[:, SMALL : 2 * SMALL], tr_scales[:, SMALL : 2 * SMALL]
             at_rep_codes = stream.tile([P, COLS], U32, align_bytes=64)
             at_rep_scales = stream.tile([P, COLS], U8, align_bytes=64)
             nc.vector.tensor_copy(
                 out=at_rep_codes[:].bitcast(I32).rearrange("p (m t x) -> p m t x", m=M, t=NT),
-                in_=at_codes[:]
+                in_=at_codes
                 .bitcast(I32)
                 .rearrange("p (m x) -> p m x", m=M)
                 .unsqueeze(2)
@@ -193,39 +232,18 @@ def tile_layer_3d_dep_pa_t_kernel(tc, A, P1, P2, P3, P4, a5, gamma, beta, out):
             )
             nc.vector.tensor_copy(
                 out=at_rep_scales[:].bitcast(I32).rearrange("p (m t x) -> p m t x", m=M, t=NT),
-                in_=at_scales[:]
+                in_=at_scales
                 .bitcast(I32)
                 .rearrange("p (m x) -> p m x", m=M)
                 .unsqueeze(2)
                 .to_broadcast([P, M, NT, KR // 4]),
             )
 
-            r_sums = single.tile([P, PACK, SMALL], F32)
-            nc.vector.tensor_reduce(
-                out=r_sums[:].rearrange("p j (x t) -> p (j x) t", t=NT),
-                in_=raw[:].rearrange("p j m (k r t) -> p (j m k) t r", r=NR, t=NT),
-                axis=AXIS_X,
-                op=ALU.add,
-            )
-            grouped_ar = stream.tile([P, SMALL, PACK], BF16, align_bytes=64)
-            nc.scalar.activation(
-                out=grouped_ar[:],
-                in_=r_sums[:].rearrange("p j x -> p x j"),
-                func=ACT.Copy,
-                scale=1.0 / NR,
-            )
-            ar_codes = stream.tile([P, SMALL], U32, align_bytes=64)
-            ar_scales = stream.tile([P, SMALL], U8, align_bytes=64)
-            nc.vector.quantize_mx(
-                out=ar_codes[:].bitcast(FP8X4),
-                scales=ar_scales[:],
-                in_=grouped_ar[:].rearrange("p w j -> p (w j)"),
-            )
 
             for ot in range(O_TILES):
                 a4_acc = psum_small.tile([P, SMALL], F32, tag="small")
-                mix(a4_acc[:], W_A4_HI, ot, ar_codes[:], ar_scales[:], True, False)
-                mix(a4_acc[:], W_A4_LO, ot, ar_codes[:], ar_scales[:], False, True)
+                mix(a4_acc[:], W_A4_HI, ot, ar_codes, ar_scales, True, False)
+                mix(a4_acc[:], W_A4_LO, ot, ar_codes, ar_scales, False, True)
                 no_r = stream.tile([P, M, K_PIECE, NT], F32)
                 nc.vector.scalar_tensor_tensor(
                     out=no_r[:].rearrange("p m k t -> p m (k t)"),

@@ -64,6 +64,10 @@ def tile_layer_3d_dep_pa_t_kernel(tc, A, P1, P2, P3, P4, a5, gamma, beta, out):
         make_identity(nc, ident_bf16[:])
         pool_mat = keep.tile([P, 2, POOLED], BF16)
 
+        table_warmer = keep.tile([P, 1], F32)
+        nc.vector.memset(table_warmer[:], 1.0)
+        nc.scalar.sqrt(out=table_warmer[:], in_=table_warmer[:])
+
         nc.sync.dma_start(
             out=a5_sb[:], in_=a5.rearrange("b (ot o) m k t -> o (b ot) (m k t)", o=P)
         )
@@ -123,9 +127,9 @@ def tile_layer_3d_dep_pa_t_kernel(tc, A, P1, P2, P3, P4, a5, gamma, beta, out):
             nc.tensor.transpose(gb_turned[:], gb_rows[:], ident_bf16[:])
             nc.vector.tensor_copy(out=gamma_beta[:], in_=gb_turned[:, 0 : 2 * O_TILES])
 
-        stream = ctx.enter_context(tc.tile_pool(name="stream", bufs=2))
-        single = ctx.enter_context(tc.tile_pool(name="single", bufs=1))
-        turned_pool = ctx.enter_context(tc.tile_pool(name="turned_pool", bufs=3))
+        once = ctx.enter_context(tc.tile_pool(name="once", bufs=1))
+        twice = ctx.enter_context(tc.tile_pool(name="twice", bufs=2))
+        thrice = ctx.enter_context(tc.tile_pool(name="thrice", bufs=3))
 
         def mix(acc, weight, ot, codes, scales, start, stop):
             nc.tensor.matmul_mx(
@@ -138,18 +142,45 @@ def tile_layer_3d_dep_pa_t_kernel(tc, A, P1, P2, P3, P4, a5, gamma, beta, out):
                 stop=stop,
             )
 
-        for piece in range(N_PIECES):
+        def load(piece):
             b, kq = divmod(piece, PIECES_PER_B)
-
-            raw = stream.tile([P, PACK, M, RUN], BF16)
+            raw = thrice.tile([P, PACK, M, RUN], BF16, name="raw")
             nc.sync.dma_start(
                 out=raw[:],
                 in_=A[b].rearrange("(p j) m k r t -> p j m (k r t)", j=PACK)[
                     :, :, :, kq * RUN : (kq + 1) * RUN
                 ],
             )
+            return raw
 
-            grouped_a = stream.tile([P, COLS, PACK], BF16, align_bytes=64)
+        def front(raw):
+            pooled = [
+                psum_pooled.tile([P, 2, PACK, 2, HALVES, POOLED], F32, name="pooled%d" % i, tag="pooled")
+                for i in range(M // 2)
+            ]
+            turned = {}
+            for j in range(PACK + 1):
+                if j < PACK:
+                    turned_ps = psum_turned.tile([P, M, HALVES, P], BF16, name="turned_ps")
+                    for m in range(M):
+                        for h in range(HALVES):
+                            nc.tensor.transpose(
+                                turned_ps[:, m, h, :], raw[:, j, m, h * P : (h + 1) * P], ident_bf16[:]
+                            )
+                    turned[j] = twice.tile([P, M, HALVES, P], BF16, name="turned")
+                    nc.scalar.copy(out=turned[j][:], in_=turned_ps[:])
+                if j > 0:
+                    for m in range(M):
+                        for h in range(HALVES):
+                            nc.tensor.matmul(
+                                out=pooled[m // 2][:, :, j - 1, m % 2, h, :],
+                                lhsT=turned[j - 1][:, m, h, :],
+                                rhs=pool_mat[:],
+                                start=True,
+                                stop=True,
+                            )
+
+            grouped_a = once.tile([P, COLS, PACK], BF16, align_bytes=64, name="grouped_a")
             for m in range(M):
                 nc.vector.tensor_copy(
                     out=grouped_a[:, m * RUN : (m + 1) * RUN, :].rearrange(
@@ -157,74 +188,52 @@ def tile_layer_3d_dep_pa_t_kernel(tc, A, P1, P2, P3, P4, a5, gamma, beta, out):
                     ),
                     in_=raw[:, :, m, :].rearrange("p j (x t) -> p t x j", t=NT),
                 )
-            a_codes = stream.tile([P, COLS], U32, align_bytes=64)
-            a_scales = stream.tile([P, COLS], U8, align_bytes=64)
+            pair_sums = once.tile([P, PACK, 2, RUN], F32, name="pair_sums")
+            nc.vector.tensor_add(out=pair_sums[:], in0=raw[:, :, 0:2, :], in1=raw[:, :, 2:4, :])
+            m_sums = once.tile([P, PACK, RUN], F32, name="m_sums")
+            nc.vector.tensor_add(out=m_sums[:], in0=pair_sums[:, :, 0, :], in1=pair_sums[:, :, 1, :])
+            a_codes = twice.tile([P, COLS], U32, align_bytes=64, name="a_codes")
+            a_scales = twice.tile([P, COLS], U8, align_bytes=64, name="a_scales")
             nc.vector.quantize_mx(
                 out=a_codes[:].bitcast(FP8X4),
                 scales=a_scales[:],
                 in_=grouped_a[:].rearrange("p w j -> p (w j)"),
             )
 
-            pair_sums = single.tile([P, PACK, 2, RUN], F32)
-            nc.vector.tensor_add(out=pair_sums[:], in0=raw[:, :, 0:2, :], in1=raw[:, :, 2:4, :])
-            m_sums = single.tile([P, PACK, RUN], F32)
-            nc.vector.tensor_add(out=m_sums[:], in0=pair_sums[:, :, 0, :], in1=pair_sums[:, :, 1, :])
-            grouped_am = stream.tile([P, RUN, PACK], BF16, align_bytes=64)
+            grouped_tr = once.tile([P, 2, SMALL, PACK], BF16, align_bytes=64, name="grouped_tr")
+            for i in range(M // 2):
+                nc.scalar.copy(
+                    out=grouped_tr[:, :, i * (SMALL // 2) : (i + 1) * (SMALL // 2), :],
+                    in_=pooled[i][:].rearrange("p s j m h x -> p s (m h x) j"),
+                )
+            grouped_am = once.tile([P, RUN, PACK], BF16, align_bytes=64, name="grouped_am")
             nc.scalar.activation(
                 out=grouped_am[:].rearrange("p (t x) j -> p t x j", t=NT),
                 in_=m_sums[:].rearrange("p j (x t) -> p t x j", t=NT),
                 func=ACT.Copy,
                 scale=1.0 / M,
             )
-            am_codes = stream.tile([P, RUN], U32, align_bytes=64)
-            am_scales = stream.tile([P, RUN], U8, align_bytes=64)
+            return {"a": (a_codes, a_scales), "grouped_am": grouped_am, "grouped_tr": grouped_tr}
+
+        def back(ops):
+            am_codes = twice.tile([P, RUN], U32, align_bytes=64, name="am_codes")
+            am_scales = twice.tile([P, RUN], U8, align_bytes=64, name="am_scales")
             nc.vector.quantize_mx(
                 out=am_codes[:].bitcast(FP8X4),
                 scales=am_scales[:],
-                in_=grouped_am[:].rearrange("p w j -> p (w j)"),
+                in_=ops["grouped_am"][:].rearrange("p w j -> p (w j)"),
             )
-
-            pooled = [
-                psum_pooled.tile([P, 2, PACK, 2, HALVES, POOLED], F32, name="pooled%d" % i, tag="pooled")
-                for i in range(M // 2)
-            ]
-            for j in range(PACK):
-                turned_ps = psum_turned.tile([P, M, HALVES, P], BF16)
-                for m in range(M):
-                    for h in range(HALVES):
-                        nc.tensor.transpose(
-                            turned_ps[:, m, h, :], raw[:, j, m, h * P : (h + 1) * P], ident_bf16[:]
-                        )
-                turned = turned_pool.tile([P, M, HALVES, P], BF16)
-                nc.scalar.copy(out=turned[:], in_=turned_ps[:])
-                for m in range(M):
-                    for h in range(HALVES):
-                        nc.tensor.matmul(
-                            out=pooled[m // 2][:, :, j, m % 2, h, :],
-                            lhsT=turned[:, m, h, :],
-                            rhs=pool_mat[:],
-                            start=True,
-                            stop=True,
-                        )
-            grouped_tr = stream.tile([P, 2, SMALL, PACK], BF16, align_bytes=64)
-            for i in range(M // 2):
-                nc.scalar.copy(
-                    out=grouped_tr[:, :, i * (SMALL // 2) : (i + 1) * (SMALL // 2), :],
-                    in_=pooled[i][:].rearrange("p s j m h x -> p s (m h x) j"),
-                )
-            tr_codes = stream.tile([P, 2 * SMALL], U32, align_bytes=64)
+            tr_codes = twice.tile([P, 2 * SMALL], U32, align_bytes=64, name="tr_codes")
             nc.vector.quantize_mx(
                 out=tr_codes[:].bitcast(FP8X4),
                 scales=tr_scales[:],
-                in_=grouped_tr[:].rearrange("p s w j -> p (s w j)"),
+                in_=ops["grouped_tr"][:].rearrange("p s w j -> p (s w j)"),
             )
-            at_codes, at_scales = tr_codes[:, 0:SMALL], tr_scales[:, 0:SMALL]
-            ar_codes, ar_scales = tr_codes[:, SMALL : 2 * SMALL], tr_scales[:, SMALL : 2 * SMALL]
-            at_rep_codes = stream.tile([P, COLS], U32, align_bytes=64)
-            at_rep_scales = stream.tile([P, COLS], U8, align_bytes=64)
+            at_rep_codes = twice.tile([P, COLS], U32, align_bytes=64, name="at_rep_codes")
+            at_rep_scales = twice.tile([P, COLS], U8, align_bytes=64, name="at_rep_scales")
             nc.vector.tensor_copy(
                 out=at_rep_codes[:].bitcast(I32).rearrange("p (m t x) -> p m t x", m=M, t=NT),
-                in_=at_codes
+                in_=tr_codes[:, 0:SMALL]
                 .bitcast(I32)
                 .rearrange("p (m x) -> p m x", m=M)
                 .unsqueeze(2)
@@ -232,35 +241,45 @@ def tile_layer_3d_dep_pa_t_kernel(tc, A, P1, P2, P3, P4, a5, gamma, beta, out):
             )
             nc.vector.tensor_copy(
                 out=at_rep_scales[:].bitcast(I32).rearrange("p (m t x) -> p m t x", m=M, t=NT),
-                in_=at_scales
+                in_=tr_scales[:, 0:SMALL]
                 .bitcast(I32)
                 .rearrange("p (m x) -> p m x", m=M)
                 .unsqueeze(2)
                 .to_broadcast([P, M, NT, KR // 4]),
             )
+            ops["am"] = (am_codes, am_scales)
+            ops["at_rep"] = (at_rep_codes, at_rep_scales)
+            ops["ar"] = (tr_codes[:, SMALL : 2 * SMALL], tr_scales[:, SMALL : 2 * SMALL])
 
-
+        def mixes(piece, ops):
+            b, kq = divmod(piece, PIECES_PER_B)
+            a_codes, a_scales = ops["a"]
+            am_codes, am_scales = ops["am"]
+            at_rep_codes, at_rep_scales = ops["at_rep"]
+            ar_codes, ar_scales = ops["ar"]
+            a4_acc = psum_small.tile([P, O_TILES, SMALL], F32, tag="small", name="a4_acc")
+            no_r = twice.tile([P, O_TILES, M, K_PIECE, NT], F32, name="no_r")
             for ot in range(O_TILES):
-                a4_acc = psum_small.tile([P, SMALL], F32, tag="small")
-                mix(a4_acc[:], W_A4_HI, ot, ar_codes, ar_scales, True, False)
-                mix(a4_acc[:], W_A4_LO, ot, ar_codes, ar_scales, False, True)
-                no_r = stream.tile([P, M, K_PIECE, NT], F32)
+                mix(a4_acc[:, ot, :], W_A4_HI, ot, ar_codes, ar_scales, True, False)
+                mix(a4_acc[:, ot, :], W_A4_LO, ot, ar_codes, ar_scales, False, True)
+            for ot in range(O_TILES):
                 nc.vector.scalar_tensor_tensor(
-                    out=no_r[:].rearrange("p m k t -> p m (k t)"),
+                    out=no_r[:, ot].rearrange("p m k t -> p m (k t)"),
                     in0=a5_sb[:, b * O_TILES + ot, :].rearrange(
                         "p (m kq x) -> p m kq x", m=M, kq=PIECES_PER_B
                     )[:, :, kq, :],
                     scalar=2.0 * UP,
-                    in1=a4_acc[:].rearrange("p (m x) -> p m x", m=M),
+                    in1=a4_acc[:, ot, :].rearrange("p (m x) -> p m x", m=M),
                     op0=ALU.mult,
                     op1=ALU.add,
                 )
 
+            for ot in range(O_TILES):
                 y_piece = y[:, ot, b, :].rearrange("p (m kq x) -> p m kq x", m=M, kq=PIECES_PER_B)[
                     :, :, kq, :
                 ]
                 for m0 in range(0, M, 2):
-                    acc = psum_x.tile([P, 2, RUN], F32)
+                    acc = psum_x.tile([P, 2, RUN], F32, name="acc")
                     for i in range(2):
                         cols = slice((m0 + i) * RUN, (m0 + i + 1) * RUN)
                         mix(acc[:, i, :], W_A1_HI, ot, a_codes[:, cols], a_scales[:, cols], True, False)
@@ -275,41 +294,63 @@ def tile_layer_3d_dep_pa_t_kernel(tc, A, P1, P2, P3, P4, a5, gamma, beta, out):
                             "p m (k r t) -> p m k r t", r=NR, t=NT
                         ),
                         in0=acc[:].rearrange("p m (t k r) -> p m k r t", t=NT, r=NR),
-                        in1=no_r[:, m0 : m0 + 2, :, :]
+                        in1=no_r[:, ot, m0 : m0 + 2, :, :]
                         .unsqueeze(3)
                         .to_broadcast([P, 2, K_PIECE, NR, NT]),
                         op=ALU.add,
                     )
 
+        def activate(piece):
+            b, kq = divmod(piece, PIECES_PER_B)
+            for ot in range(O_TILES):
+                y_piece = y[:, ot, b, :].rearrange("p (m kq x) -> p m kq x", m=M, kq=PIECES_PER_B)[
+                    :, :, kq, :
+                ]
                 nc.scalar.activation(
                     out=y_piece, in_=y_piece, func=ACT.Relu,
                     accum_out=sums[:, ot, piece : piece + 1],
                 )
-                squared = stream.tile([P, M, RUN], BF16)
+                squared = twice.tile([P, M, RUN], BF16, name="squared")
                 nc.scalar.activation(
                     out=squared[:], in_=y_piece, func=ACT.Square,
                     accum_out=squares[:, ot, piece : piece + 1],
                 )
 
+        with tc.manual_schedule():
+            raws = {0: load(0), 1: load(1)}
+            operands = {0: front(raws[0])}
+            back(operands[0])
+            for piece in range(N_PIECES):
+                if piece + 2 < N_PIECES:
+                    raws[piece + 2] = load(piece + 2)
+                if piece + 1 < N_PIECES:
+                    operands[piece + 1] = front(raws[piece + 1])
+                if piece > 0:
+                    activate(piece - 1)
+                mixes(piece, operands[piece])
+                if piece + 1 < N_PIECES:
+                    back(operands[piece + 1])
+            activate(N_PIECES - 1)
+
         count = float(B * POSITIONS)
-        mean = single.tile([P, O_TILES], F32)
+        mean = once.tile([P, O_TILES], F32)
         nc.vector.tensor_reduce(out=mean[:], in_=sums[:], axis=AXIS_X, op=ALU.add)
         nc.vector.tensor_scalar_mul(out=mean[:], in0=mean[:], scalar1=1.0 / count)
-        var = single.tile([P, O_TILES], F32)
+        var = once.tile([P, O_TILES], F32)
         nc.vector.tensor_reduce(out=var[:], in_=squares[:], axis=AXIS_X, op=ALU.add)
         nc.vector.tensor_scalar_mul(out=var[:], in0=var[:], scalar1=1.0 / count)
-        mean_sq = single.tile([P, O_TILES], F32)
+        mean_sq = once.tile([P, O_TILES], F32)
         nc.vector.tensor_mul(out=mean_sq[:], in0=mean[:], in1=mean[:])
         nc.vector.tensor_sub(out=var[:], in0=var[:], in1=mean_sq[:])
         nc.vector.tensor_scalar(
             out=var[:], in0=var[:], scalar1=0.0, scalar2=BN_EPS * UP * UP, op0=ALU.max, op1=ALU.add
         )
-        std = single.tile([P, O_TILES], F32)
+        std = once.tile([P, O_TILES], F32)
         nc.scalar.sqrt(out=std[:], in_=var[:])
-        gain = single.tile([P, O_TILES], F32)
+        gain = once.tile([P, O_TILES], F32)
         nc.vector.reciprocal(out=gain[:], in_=std[:])
         nc.vector.tensor_mul(out=gain[:], in0=gain[:], in1=gamma_beta[:, 0:O_TILES])
-        shift = single.tile([P, O_TILES], F32)
+        shift = once.tile([P, O_TILES], F32)
         nc.vector.tensor_mul(out=shift[:], in0=mean[:], in1=gain[:])
         nc.vector.tensor_sub(out=shift[:], in0=gamma_beta[:, O_TILES : 2 * O_TILES], in1=shift[:])
 

@@ -29,6 +29,7 @@ COLS = M * RUN
 SMALL = M * KR
 HALVES = RUN // P
 K_SQUARE = K_PIECE // HALVES
+T_RUN = 4
 POOLED = K_SQUARE * NR
 
 UP = 10.0
@@ -181,12 +182,12 @@ def tile_layer_3d_dep_pa_t_kernel(tc, A, P1, P2, P3, P4, a5, gamma, beta, out):
                             )
 
             grouped_a = once.tile([P, COLS, PACK], BF16, align_bytes=64, name="grouped_a")
-            for m in range(M):
+            for th in range(NT // T_RUN):
                 nc.vector.tensor_copy(
-                    out=grouped_a[:, m * RUN : (m + 1) * RUN, :].rearrange(
-                        "p (t x) j -> p t x j", t=NT
-                    ),
-                    in_=raw[:, :, m, :].rearrange("p j (x t) -> p t x j", t=NT),
+                    out=grouped_a[:].rearrange(
+                        "p (m th tl x) j -> p th m x j tl", m=M, tl=T_RUN, x=KR
+                    )[:, th],
+                    in_=raw[:].rearrange("p j m (x th tl) -> p th m x j tl", x=KR, tl=T_RUN)[:, th],
                 )
             pair_sums = once.tile([P, PACK, 2, RUN], F32, name="pair_sums")
             nc.vector.tensor_add(out=pair_sums[:], in0=raw[:, :, 0:2, :], in1=raw[:, :, 2:4, :])

@@ -36,8 +36,6 @@ UP = 10.0
 STATIONARY = (("p1", 8.0), ("p1", 2.0), ("p2", 1.0), ("p3", 1.0), ("p4", 4.0), ("p4", 1.0))
 W_A1_HI, W_A1_LO, W_A2, W_A3, W_A4_HI, W_A4_LO = 0, 1, 2, 3, 4, 5
 
-STORE_COLS = 2048
-
 FLOPS = 2 * O * C * B * POSITIONS * (8 + 2 + 1 + 1) // 8
 
 
@@ -56,7 +54,7 @@ def tile_layer_3d_dep_pa_t_kernel(tc, A, P1, P2, P3, P4, a5, gamma, beta, out):
         w_scales = keep.tile([P, len(STATIONARY), O], U8, align_bytes=64)
         a5_sb = keep.tile([P, B * O_TILES, M * K * NT], BF16)
         gamma_beta = keep.tile([P, 2 * O_TILES], F32)
-        y = keep.tile([P, O_TILES, B, POSITIONS], F32)
+        y = keep.tile([P, O_TILES, N_PIECES, COLS], F32)
         sums = keep.tile([P, O_TILES, N_PIECES], F32)
         squares = keep.tile([P, O_TILES, N_PIECES], F32)
         tr_scales = keep.tile([P, 2 * SMALL], U8, align_bytes=64)
@@ -69,9 +67,20 @@ def tile_layer_3d_dep_pa_t_kernel(tc, A, P1, P2, P3, P4, a5, gamma, beta, out):
         nc.vector.memset(table_warmer[:], 1.0)
         nc.scalar.sqrt(out=table_warmer[:], in_=table_warmer[:])
 
-        nc.sync.dma_start(
-            out=a5_sb[:], in_=a5.rearrange("b (ot o) m k t -> o (b ot) (m k t)", o=P)
-        )
+        raw_pool = ctx.enter_context(tc.tile_pool(name="raw_pool", bufs=2))
+
+        def load(piece):
+            b, kq = divmod(piece, PIECES_PER_B)
+            raw = raw_pool.tile([P, PACK, M, RUN], BF16, name="raw")
+            nc.sync.dma_start(
+                out=raw[:],
+                in_=A[b].rearrange("(p j) m k r t -> p j m (k r t)", j=PACK)[
+                    :, :, :, kq * RUN : (kq + 1) * RUN
+                ],
+            )
+            return raw
+
+        raws = {0: load(0)}
 
         with tc.tile_pool(name="setup", bufs=2) as setup:
             ident_f32 = setup.tile([P, P], F32, tag="ident_f32")
@@ -128,248 +137,240 @@ def tile_layer_3d_dep_pa_t_kernel(tc, A, P1, P2, P3, P4, a5, gamma, beta, out):
             nc.tensor.transpose(gb_turned[:], gb_rows[:], ident_bf16[:])
             nc.vector.tensor_copy(out=gamma_beta[:], in_=gb_turned[:, 0 : 2 * O_TILES])
 
-        once = ctx.enter_context(tc.tile_pool(name="once", bufs=1))
-        twice = ctx.enter_context(tc.tile_pool(name="twice", bufs=2))
-        thrice = ctx.enter_context(tc.tile_pool(name="thrice", bufs=3))
+        raws[1] = load(1)
+        nc.sync.dma_start(
+            out=a5_sb[:], in_=a5.rearrange("b (ot o) m k t -> o (b ot) (m k t)", o=P)
+        )
 
-        def mix(acc, weight, ot, codes, scales, start, stop):
-            nc.tensor.matmul_mx(
-                out=acc,
-                lhsT=w_codes[:, weight, ot * P : (ot + 1) * P].bitcast(FP8X4),
-                lhsT_scale=w_scales[:, weight, ot * P : (ot + 1) * P],
-                rhs=codes.bitcast(FP8X4),
-                rhs_scale=scales,
-                start=start,
-                stop=stop,
-            )
+        with tc.tile_pool(name="once", bufs=1) as once, tc.tile_pool(name="twice", bufs=2) as twice:
 
-        def load(piece):
-            b, kq = divmod(piece, PIECES_PER_B)
-            raw = thrice.tile([P, PACK, M, RUN], BF16, name="raw")
-            nc.sync.dma_start(
-                out=raw[:],
-                in_=A[b].rearrange("(p j) m k r t -> p j m (k r t)", j=PACK)[
-                    :, :, :, kq * RUN : (kq + 1) * RUN
-                ],
-            )
-            return raw
-
-        def front(raw):
-            pooled = [
-                psum_pooled.tile([P, 2, PACK, 2, HALVES, POOLED], F32, name="pooled%d" % i, tag="pooled")
-                for i in range(M // 2)
-            ]
-            turned = {}
-            for j in range(PACK + 1):
-                if j < PACK:
-                    turned_ps = psum_turned.tile([P, M, HALVES, P], BF16, name="turned_ps")
-                    for m in range(M):
-                        for h in range(HALVES):
-                            nc.tensor.transpose(
-                                turned_ps[:, m, h, :], raw[:, j, m, h * P : (h + 1) * P], ident_bf16[:]
-                            )
-                    turned[j] = twice.tile([P, M, HALVES, P], BF16, name="turned")
-                    nc.scalar.copy(out=turned[j][:], in_=turned_ps[:])
-                if j > 0:
-                    for m in range(M):
-                        for h in range(HALVES):
-                            nc.tensor.matmul(
-                                out=pooled[m // 2][:, :, j - 1, m % 2, h, :],
-                                lhsT=turned[j - 1][:, m, h, :],
-                                rhs=pool_mat[:],
-                                start=True,
-                                stop=True,
-                            )
-
-            grouped_a = once.tile([P, COLS, PACK], BF16, align_bytes=64, name="grouped_a")
-            for th in range(NT // T_RUN):
-                nc.vector.tensor_copy(
-                    out=grouped_a[:].rearrange(
-                        "p (m th tl x) j -> p th m x j tl", m=M, tl=T_RUN, x=KR
-                    )[:, th],
-                    in_=raw[:].rearrange("p j m (x th tl) -> p th m x j tl", x=KR, tl=T_RUN)[:, th],
-                )
-            pair_sums = once.tile([P, PACK, 2, RUN], F32, name="pair_sums")
-            nc.vector.tensor_add(out=pair_sums[:], in0=raw[:, :, 0:2, :], in1=raw[:, :, 2:4, :])
-            m_sums = once.tile([P, PACK, RUN], F32, name="m_sums")
-            nc.vector.tensor_add(out=m_sums[:], in0=pair_sums[:, :, 0, :], in1=pair_sums[:, :, 1, :])
-            a_codes = twice.tile([P, COLS], U32, align_bytes=64, name="a_codes")
-            a_scales = twice.tile([P, COLS], U8, align_bytes=64, name="a_scales")
-            nc.vector.quantize_mx(
-                out=a_codes[:].bitcast(FP8X4),
-                scales=a_scales[:],
-                in_=grouped_a[:].rearrange("p w j -> p (w j)"),
-            )
-
-            grouped_tr = once.tile([P, 2, SMALL, PACK], BF16, align_bytes=64, name="grouped_tr")
-            for i in range(M // 2):
-                nc.scalar.copy(
-                    out=grouped_tr[:, :, i * (SMALL // 2) : (i + 1) * (SMALL // 2), :],
-                    in_=pooled[i][:].rearrange("p s j m h x -> p s (m h x) j"),
-                )
-            grouped_am = once.tile([P, RUN, PACK], BF16, align_bytes=64, name="grouped_am")
-            nc.scalar.activation(
-                out=grouped_am[:].rearrange("p (t x) j -> p t x j", t=NT),
-                in_=m_sums[:].rearrange("p j (x t) -> p t x j", t=NT),
-                func=ACT.Copy,
-                scale=1.0 / M,
-            )
-            return {"a": (a_codes, a_scales), "grouped_am": grouped_am, "grouped_tr": grouped_tr}
-
-        def back(ops):
-            am_codes = twice.tile([P, RUN], U32, align_bytes=64, name="am_codes")
-            am_scales = twice.tile([P, RUN], U8, align_bytes=64, name="am_scales")
-            nc.vector.quantize_mx(
-                out=am_codes[:].bitcast(FP8X4),
-                scales=am_scales[:],
-                in_=ops["grouped_am"][:].rearrange("p w j -> p (w j)"),
-            )
-            tr_codes = twice.tile([P, 2 * SMALL], U32, align_bytes=64, name="tr_codes")
-            nc.vector.quantize_mx(
-                out=tr_codes[:].bitcast(FP8X4),
-                scales=tr_scales[:],
-                in_=ops["grouped_tr"][:].rearrange("p s w j -> p (s w j)"),
-            )
-            at_rep_codes = twice.tile([P, COLS], U32, align_bytes=64, name="at_rep_codes")
-            at_rep_scales = twice.tile([P, COLS], U8, align_bytes=64, name="at_rep_scales")
-            nc.vector.tensor_copy(
-                out=at_rep_codes[:].bitcast(I32).rearrange("p (m t x) -> p m t x", m=M, t=NT),
-                in_=tr_codes[:, 0:SMALL]
-                .bitcast(I32)
-                .rearrange("p (m x) -> p m x", m=M)
-                .unsqueeze(2)
-                .to_broadcast([P, M, NT, KR]),
-            )
-            nc.vector.tensor_copy(
-                out=at_rep_scales[:].bitcast(I32).rearrange("p (m t x) -> p m t x", m=M, t=NT),
-                in_=tr_scales[:, 0:SMALL]
-                .bitcast(I32)
-                .rearrange("p (m x) -> p m x", m=M)
-                .unsqueeze(2)
-                .to_broadcast([P, M, NT, KR // 4]),
-            )
-            ops["am"] = (am_codes, am_scales)
-            ops["at_rep"] = (at_rep_codes, at_rep_scales)
-            ops["ar"] = (tr_codes[:, SMALL : 2 * SMALL], tr_scales[:, SMALL : 2 * SMALL])
-
-        def mixes(piece, ops):
-            b, kq = divmod(piece, PIECES_PER_B)
-            a_codes, a_scales = ops["a"]
-            am_codes, am_scales = ops["am"]
-            at_rep_codes, at_rep_scales = ops["at_rep"]
-            ar_codes, ar_scales = ops["ar"]
-            a4_acc = psum_small.tile([P, O_TILES, SMALL], F32, tag="small", name="a4_acc")
-            no_r = twice.tile([P, O_TILES, M, K_PIECE, NT], F32, name="no_r")
-            for ot in range(O_TILES):
-                mix(a4_acc[:, ot, :], W_A4_HI, ot, ar_codes, ar_scales, True, False)
-                mix(a4_acc[:, ot, :], W_A4_LO, ot, ar_codes, ar_scales, False, True)
-            for ot in range(O_TILES):
-                nc.vector.scalar_tensor_tensor(
-                    out=no_r[:, ot].rearrange("p m k t -> p m (k t)"),
-                    in0=a5_sb[:, b * O_TILES + ot, :].rearrange(
-                        "p (m kq x) -> p m kq x", m=M, kq=PIECES_PER_B
-                    )[:, :, kq, :],
-                    scalar=2.0 * UP,
-                    in1=a4_acc[:, ot, :].rearrange("p (m x) -> p m x", m=M),
-                    op0=ALU.mult,
-                    op1=ALU.add,
+            def mix(acc, weight, ot, codes, scales, start, stop):
+                nc.tensor.matmul_mx(
+                    out=acc,
+                    lhsT=w_codes[:, weight, ot * P : (ot + 1) * P].bitcast(FP8X4),
+                    lhsT_scale=w_scales[:, weight, ot * P : (ot + 1) * P],
+                    rhs=codes.bitcast(FP8X4),
+                    rhs_scale=scales,
+                    start=start,
+                    stop=stop,
                 )
 
-            for ot in range(O_TILES):
-                y_piece = y[:, ot, b, :].rearrange("p (m kq x) -> p m kq x", m=M, kq=PIECES_PER_B)[
-                    :, :, kq, :
+            def front(raw):
+                pooled = [
+                    psum_pooled.tile([P, 2, PACK, 2, HALVES, POOLED], F32, name="pooled%d" % i, tag="pooled")
+                    for i in range(M // 2)
                 ]
-                for m0 in range(0, M, 2):
-                    acc = psum_x.tile([P, 2, RUN], F32, name="acc")
-                    for i in range(2):
-                        cols = slice((m0 + i) * RUN, (m0 + i + 1) * RUN)
-                        mix(acc[:, i, :], W_A1_HI, ot, a_codes[:, cols], a_scales[:, cols], True, False)
-                        mix(acc[:, i, :], W_A1_LO, ot, a_codes[:, cols], a_scales[:, cols], False, False)
-                        mix(acc[:, i, :], W_A2, ot, am_codes[:], am_scales[:], False, False)
-                        mix(
-                            acc[:, i, :], W_A3, ot, at_rep_codes[:, cols], at_rep_scales[:, cols],
-                            False, True,
-                        )
-                    nc.vector.tensor_tensor(
-                        out=y_piece[:, m0 : m0 + 2, :].rearrange(
-                            "p m (k r t) -> p m k r t", r=NR, t=NT
-                        ),
-                        in0=acc[:].rearrange("p m (t k r) -> p m k r t", t=NT, r=NR),
-                        in1=no_r[:, ot, m0 : m0 + 2, :, :]
-                        .unsqueeze(3)
-                        .to_broadcast([P, 2, K_PIECE, NR, NT]),
-                        op=ALU.add,
+                turned = {}
+                for j in range(PACK + 1):
+                    if j < PACK:
+                        turned_ps = psum_turned.tile([P, M, HALVES, P], BF16, name="turned_ps")
+                        for m in range(M):
+                            for h in range(HALVES):
+                                nc.tensor.transpose(
+                                    turned_ps[:, m, h, :], raw[:, j, m, h * P : (h + 1) * P], ident_bf16[:]
+                                )
+                        turned[j] = twice.tile([P, M, HALVES, P], BF16, name="turned")
+                        nc.scalar.copy(out=turned[j][:], in_=turned_ps[:])
+                    if j > 0:
+                        for m in range(M):
+                            for h in range(HALVES):
+                                nc.tensor.matmul(
+                                    out=pooled[m // 2][:, :, j - 1, m % 2, h, :],
+                                    lhsT=turned[j - 1][:, m, h, :],
+                                    rhs=pool_mat[:],
+                                    start=True,
+                                    stop=True,
+                                )
+
+                grouped_a = once.tile([P, COLS, PACK], BF16, align_bytes=64, name="grouped_a")
+                for th in range(NT // T_RUN):
+                    nc.vector.tensor_copy(
+                        out=grouped_a[:].rearrange(
+                            "p (m th tl x) j -> p th m x j tl", m=M, tl=T_RUN, x=KR
+                        )[:, th],
+                        in_=raw[:].rearrange("p j m (x th tl) -> p th m x j tl", x=KR, tl=T_RUN)[:, th],
+                    )
+                pair_sums = once.tile([P, PACK, 2, RUN], F32, name="pair_sums")
+                nc.vector.tensor_add(out=pair_sums[:], in0=raw[:, :, 0:2, :], in1=raw[:, :, 2:4, :])
+                m_sums = once.tile([P, PACK, RUN], F32, name="m_sums")
+                nc.vector.tensor_add(out=m_sums[:], in0=pair_sums[:, :, 0, :], in1=pair_sums[:, :, 1, :])
+                a_codes = twice.tile([P, COLS], U32, align_bytes=64, name="a_codes")
+                a_scales = twice.tile([P, COLS], U8, align_bytes=64, name="a_scales")
+                nc.vector.quantize_mx(
+                    out=a_codes[:].bitcast(FP8X4),
+                    scales=a_scales[:],
+                    in_=grouped_a[:].rearrange("p w j -> p (w j)"),
+                )
+
+                grouped_tr = once.tile([P, 2, SMALL, PACK], BF16, align_bytes=64, name="grouped_tr")
+                for i in range(M // 2):
+                    nc.scalar.copy(
+                        out=grouped_tr[:, :, i * (SMALL // 2) : (i + 1) * (SMALL // 2), :],
+                        in_=pooled[i][:].rearrange("p s j m h x -> p s (m h x) j"),
+                    )
+                grouped_am = once.tile([P, RUN, PACK], BF16, align_bytes=64, name="grouped_am")
+                nc.scalar.activation(
+                    out=grouped_am[:].rearrange("p (t x) j -> p t x j", t=NT),
+                    in_=m_sums[:].rearrange("p j (x t) -> p t x j", t=NT),
+                    func=ACT.Copy,
+                    scale=1.0 / M,
+                )
+                return {"a": (a_codes, a_scales), "grouped_am": grouped_am, "grouped_tr": grouped_tr}
+
+            def back(ops):
+                am_codes = twice.tile([P, RUN], U32, align_bytes=64, name="am_codes")
+                am_scales = twice.tile([P, RUN], U8, align_bytes=64, name="am_scales")
+                nc.vector.quantize_mx(
+                    out=am_codes[:].bitcast(FP8X4),
+                    scales=am_scales[:],
+                    in_=ops["grouped_am"][:].rearrange("p w j -> p (w j)"),
+                )
+                tr_codes = twice.tile([P, 2 * SMALL], U32, align_bytes=64, name="tr_codes")
+                nc.vector.quantize_mx(
+                    out=tr_codes[:].bitcast(FP8X4),
+                    scales=tr_scales[:],
+                    in_=ops["grouped_tr"][:].rearrange("p s w j -> p (s w j)"),
+                )
+                at_rep_codes = twice.tile([P, COLS], U32, align_bytes=64, name="at_rep_codes")
+                at_rep_scales = twice.tile([P, COLS], U8, align_bytes=64, name="at_rep_scales")
+                nc.vector.tensor_copy(
+                    out=at_rep_codes[:].bitcast(I32).rearrange("p (m t x) -> p m t x", m=M, t=NT),
+                    in_=tr_codes[:, 0:SMALL]
+                    .bitcast(I32)
+                    .rearrange("p (m x) -> p m x", m=M)
+                    .unsqueeze(2)
+                    .to_broadcast([P, M, NT, KR]),
+                )
+                nc.vector.tensor_copy(
+                    out=at_rep_scales[:].bitcast(I32).rearrange("p (m t x) -> p m t x", m=M, t=NT),
+                    in_=tr_scales[:, 0:SMALL]
+                    .bitcast(I32)
+                    .rearrange("p (m x) -> p m x", m=M)
+                    .unsqueeze(2)
+                    .to_broadcast([P, M, NT, KR // 4]),
+                )
+                ops["am"] = (am_codes, am_scales)
+                ops["at_rep"] = (at_rep_codes, at_rep_scales)
+                ops["ar"] = (tr_codes[:, SMALL : 2 * SMALL], tr_scales[:, SMALL : 2 * SMALL])
+
+            def mixes(piece, ops):
+                b, kq = divmod(piece, PIECES_PER_B)
+                a_codes, a_scales = ops["a"]
+                am_codes, am_scales = ops["am"]
+                at_rep_codes, at_rep_scales = ops["at_rep"]
+                ar_codes, ar_scales = ops["ar"]
+                a4_acc = psum_small.tile([P, O_TILES, SMALL], F32, tag="small", name="a4_acc")
+                no_r = twice.tile([P, O_TILES, M, K_PIECE, NT], F32, name="no_r")
+                for ot in range(O_TILES):
+                    mix(a4_acc[:, ot, :], W_A4_HI, ot, ar_codes, ar_scales, True, False)
+                    mix(a4_acc[:, ot, :], W_A4_LO, ot, ar_codes, ar_scales, False, True)
+                for ot in range(O_TILES):
+                    nc.vector.scalar_tensor_tensor(
+                        out=no_r[:, ot].rearrange("p m k t -> p m (k t)"),
+                        in0=a5_sb[:, b * O_TILES + ot, :].rearrange(
+                            "p (m kq x) -> p m kq x", m=M, kq=PIECES_PER_B
+                        )[:, :, kq, :],
+                        scalar=2.0 * UP,
+                        in1=a4_acc[:, ot, :].rearrange("p (m x) -> p m x", m=M),
+                        op0=ALU.mult,
+                        op1=ALU.add,
                     )
 
-        def activate(piece):
-            b, kq = divmod(piece, PIECES_PER_B)
-            for ot in range(O_TILES):
-                y_piece = y[:, ot, b, :].rearrange("p (m kq x) -> p m kq x", m=M, kq=PIECES_PER_B)[
-                    :, :, kq, :
-                ]
-                nc.scalar.activation(
-                    out=y_piece, in_=y_piece, func=ACT.Relu,
-                    accum_out=sums[:, ot, piece : piece + 1],
-                )
-                squared = twice.tile([P, M, RUN], BF16, name="squared")
-                nc.scalar.activation(
-                    out=squared[:], in_=y_piece, func=ACT.Square,
-                    accum_out=squares[:, ot, piece : piece + 1],
-                )
+                for ot in range(O_TILES):
+                    for m0 in range(0, M, 2):
+                        acc = psum_x.tile([P, 2, RUN], F32, name="acc")
+                        for i in range(2):
+                            cols = slice((m0 + i) * RUN, (m0 + i + 1) * RUN)
+                            mix(acc[:, i, :], W_A1_HI, ot, a_codes[:, cols], a_scales[:, cols], True, False)
+                            mix(acc[:, i, :], W_A1_LO, ot, a_codes[:, cols], a_scales[:, cols], False, False)
+                            mix(acc[:, i, :], W_A2, ot, am_codes[:], am_scales[:], False, False)
+                            mix(
+                                acc[:, i, :], W_A3, ot, at_rep_codes[:, cols], at_rep_scales[:, cols],
+                                False, True,
+                            )
+                        for i in range(2):
+                            cols = slice((m0 + i) * RUN, (m0 + i + 1) * RUN)
+                            nc.vector.tensor_tensor(
+                                out=y[:, ot, piece, cols].rearrange("p (t k r) -> p t k r", t=NT, r=NR),
+                                in0=acc[:, i, :].rearrange("p (t k r) -> p t k r", t=NT, r=NR),
+                                in1=no_r[:, ot, m0 + i, :, :]
+                                .rearrange("p k t -> p t k")
+                                .unsqueeze(3)
+                                .to_broadcast([P, NT, K_PIECE, NR]),
+                                op=ALU.add,
+                            )
 
-        with tc.manual_schedule():
-            raws = {0: load(0), 1: load(1)}
-            operands = {0: front(raws[0])}
-            back(operands[0])
-            for piece in range(N_PIECES):
-                if piece + 2 < N_PIECES:
-                    raws[piece + 2] = load(piece + 2)
-                if piece + 1 < N_PIECES:
-                    operands[piece + 1] = front(raws[piece + 1])
-                if piece > 0:
-                    activate(piece - 1)
-                mixes(piece, operands[piece])
-                if piece + 1 < N_PIECES:
-                    back(operands[piece + 1])
-            activate(N_PIECES - 1)
+            def activate(piece):
+                for ot in range(O_TILES):
+                    y_piece = y[:, ot, piece, :]
+                    nc.scalar.activation(
+                        out=y_piece, in_=y_piece, func=ACT.Relu,
+                        accum_out=sums[:, ot, piece : piece + 1],
+                    )
+                    squared = twice.tile([P, COLS], BF16, name="squared")
+                    nc.scalar.activation(
+                        out=squared[:], in_=y_piece, func=ACT.Square,
+                        accum_out=squares[:, ot, piece : piece + 1],
+                    )
+
+            with tc.manual_schedule():
+                operands = {0: front(raws[0])}
+                back(operands[0])
+                for piece in range(N_PIECES):
+                    if piece + 2 < N_PIECES:
+                        raws[piece + 2] = load(piece + 2)
+                    if piece + 1 < N_PIECES:
+                        operands[piece + 1] = front(raws[piece + 1])
+                    if piece > 0:
+                        activate(piece - 1)
+                    mixes(piece, operands[piece])
+                    if piece + 1 < N_PIECES:
+                        back(operands[piece + 1])
+                activate(N_PIECES - 1)
 
         count = float(B * POSITIONS)
-        mean = once.tile([P, O_TILES], F32)
+        mean = keep.tile([P, O_TILES], F32)
         nc.vector.tensor_reduce(out=mean[:], in_=sums[:], axis=AXIS_X, op=ALU.add)
         nc.vector.tensor_scalar_mul(out=mean[:], in0=mean[:], scalar1=1.0 / count)
-        var = once.tile([P, O_TILES], F32)
+        var = keep.tile([P, O_TILES], F32)
         nc.vector.tensor_reduce(out=var[:], in_=squares[:], axis=AXIS_X, op=ALU.add)
         nc.vector.tensor_scalar_mul(out=var[:], in0=var[:], scalar1=1.0 / count)
-        mean_sq = once.tile([P, O_TILES], F32)
+        mean_sq = keep.tile([P, O_TILES], F32)
         nc.vector.tensor_mul(out=mean_sq[:], in0=mean[:], in1=mean[:])
         nc.vector.tensor_sub(out=var[:], in0=var[:], in1=mean_sq[:])
         nc.vector.tensor_scalar(
             out=var[:], in0=var[:], scalar1=0.0, scalar2=BN_EPS * UP * UP, op0=ALU.max, op1=ALU.add
         )
-        std = once.tile([P, O_TILES], F32)
+        std = keep.tile([P, O_TILES], F32)
         nc.scalar.sqrt(out=std[:], in_=var[:])
-        gain = once.tile([P, O_TILES], F32)
+        gain = keep.tile([P, O_TILES], F32)
         nc.vector.reciprocal(out=gain[:], in_=std[:])
         nc.vector.tensor_mul(out=gain[:], in0=gain[:], in1=gamma_beta[:, 0:O_TILES])
-        shift = once.tile([P, O_TILES], F32)
+        shift = keep.tile([P, O_TILES], F32)
         nc.vector.tensor_mul(out=shift[:], in0=mean[:], in1=gain[:])
         nc.vector.tensor_sub(out=shift[:], in0=gamma_beta[:, O_TILES : 2 * O_TILES], in1=shift[:])
 
+        staged_pool = ctx.enter_context(tc.tile_pool(name="staged_pool", bufs=4))
         step = 0
         for b in range(B):
-            out_b = out[b].rearrange("(ot o) m k r t -> o ot (m k r t)", o=P)
+            out_b = out[b].rearrange("(ot o) m k r t -> o ot m (k r t)", o=P)
             for ot in range(O_TILES):
-                for c0 in range(0, POSITIONS, STORE_COLS):
-                    part = y[:, ot, b, c0 : c0 + STORE_COLS]
+                for m in range(M):
+                    source = y[
+                        :, ot, b * PIECES_PER_B : (b + 1) * PIECES_PER_B, m * RUN : (m + 1) * RUN
+                    ].rearrange("p q (t x) -> p q x t", t=NT)
+                    staged = staged_pool.tile([P, PIECES_PER_B, KR, NT], F32)
                     if step % 2 == 0:
                         nc.vector.tensor_scalar(
-                            out=part, in0=part, scalar1=gain[:, ot : ot + 1],
+                            out=staged[:], in0=source, scalar1=gain[:, ot : ot + 1],
                             scalar2=shift[:, ot : ot + 1], op0=ALU.mult, op1=ALU.add,
                         )
                     else:
                         nc.scalar.activation(
-                            out=part, in_=part, func=ACT.Identity,
+                            out=staged[:], in_=source, func=ACT.Identity,
                             bias=shift[:, ot : ot + 1], scale=gain[:, ot : ot + 1],
                         )
-                    nc.sync.dma_start(out=out_b[:, ot, c0 : c0 + STORE_COLS], in_=part)
+                    nc.sync.dma_start(
+                        out=out_b[:, ot, m, :], in_=staged[:].rearrange("p q x t -> p (q x t)")
+                    )
                     step += 1

@@ -80,7 +80,7 @@ def tile_layer_3d_dep_pa_t_kernel(tc, A, P1, P2, P3, P4, a5, gamma, beta, out):
             )
             return raw
 
-        raws = {0: load(0)}
+        first_raws = {0: load(0)}
 
         with tc.tile_pool(name="setup", bufs=2) as setup:
             ident_f32 = setup.tile([P, P], F32, tag="ident_f32")
@@ -137,7 +137,7 @@ def tile_layer_3d_dep_pa_t_kernel(tc, A, P1, P2, P3, P4, a5, gamma, beta, out):
             nc.tensor.transpose(gb_turned[:], gb_rows[:], ident_bf16[:])
             nc.vector.tensor_copy(out=gamma_beta[:], in_=gb_turned[:, 0 : 2 * O_TILES])
 
-        raws[1] = load(1)
+        first_raws[1] = load(1)
         nc.sync.dma_start(
             out=a5_sb[:], in_=a5.rearrange("b (ot o) m k t -> o (b ot) (m k t)", o=P)
         )
@@ -155,33 +155,10 @@ def tile_layer_3d_dep_pa_t_kernel(tc, A, P1, P2, P3, P4, a5, gamma, beta, out):
                     stop=stop,
                 )
 
-            def front(raw):
-                pooled = [
-                    psum_pooled.tile([P, 2, PACK, 2, HALVES, POOLED], F32, name="pooled%d" % i, tag="pooled")
-                    for i in range(M // 2)
-                ]
-                turned = {}
-                for j in range(PACK + 1):
-                    if j < PACK:
-                        turned_ps = psum_turned.tile([P, M, HALVES, P], BF16, name="turned_ps")
-                        for m in range(M):
-                            for h in range(HALVES):
-                                nc.tensor.transpose(
-                                    turned_ps[:, m, h, :], raw[:, j, m, h * P : (h + 1) * P], ident_bf16[:]
-                                )
-                        turned[j] = twice.tile([P, M, HALVES, P], BF16, name="turned")
-                        nc.scalar.copy(out=turned[j][:], in_=turned_ps[:])
-                    if j > 0:
-                        for m in range(M):
-                            for h in range(HALVES):
-                                nc.tensor.matmul(
-                                    out=pooled[m // 2][:, :, j - 1, m % 2, h, :],
-                                    lhsT=turned[j - 1][:, m, h, :],
-                                    rhs=pool_mat[:],
-                                    start=True,
-                                    stop=True,
-                                )
+            tiles = {("raw", 0): first_raws[0], ("raw", 1): first_raws[1]}
 
+            def prepare_a(piece):
+                raw = tiles["raw", piece]
                 grouped_a = once.tile([P, COLS, PACK], BF16, align_bytes=64, name="grouped_a")
                 for th in range(NT // T_RUN):
                     nc.vector.tensor_copy(
@@ -193,7 +170,9 @@ def tile_layer_3d_dep_pa_t_kernel(tc, A, P1, P2, P3, P4, a5, gamma, beta, out):
                 pair_sums = once.tile([P, PACK, 2, RUN], F32, name="pair_sums")
                 nc.vector.tensor_add(out=pair_sums[:], in0=raw[:, :, 0:2, :], in1=raw[:, :, 2:4, :])
                 m_sums = once.tile([P, PACK, RUN], F32, name="m_sums")
-                nc.vector.tensor_add(out=m_sums[:], in0=pair_sums[:, :, 0, :], in1=pair_sums[:, :, 1, :])
+                nc.vector.tensor_add(
+                    out=m_sums[:], in0=pair_sums[:, :, 0, :], in1=pair_sums[:, :, 1, :]
+                )
                 a_codes = twice.tile([P, COLS], U32, align_bytes=64, name="a_codes")
                 a_scales = twice.tile([P, COLS], U8, align_bytes=64, name="a_scales")
                 nc.vector.quantize_mx(
@@ -201,35 +180,68 @@ def tile_layer_3d_dep_pa_t_kernel(tc, A, P1, P2, P3, P4, a5, gamma, beta, out):
                     scales=a_scales[:],
                     in_=grouped_a[:].rearrange("p w j -> p (w j)"),
                 )
+                grouped_am = once.tile([P, RUN, PACK], BF16, align_bytes=64, name="grouped_am")
+                nc.gpsimd.tensor_scalar(
+                    out=grouped_am[:].rearrange("p (t x) j -> p t x j", t=NT),
+                    in0=m_sums[:].rearrange("p j (x t) -> p t x j", t=NT),
+                    scalar1=1.0 / M,
+                    scalar2=0.0,
+                    op0=ALU.mult,
+                    op1=ALU.add,
+                )
+                tiles["grouped_am", piece] = grouped_am
+                tiles["a_codes", piece], tiles["a_scales", piece] = a_codes, a_scales
 
+            def turn(piece, j):
+                raw = tiles["raw", piece]
+                turned_ps = psum_turned.tile([P, M, HALVES, P], BF16, name="turned_ps")
+                for m in range(M):
+                    for h in range(HALVES):
+                        nc.tensor.transpose(
+                            turned_ps[:, m, h, :], raw[:, j, m, h * P : (h + 1) * P], ident_bf16[:]
+                        )
+                turned = twice.tile([P, M, HALVES, P], BF16, name="turned")
+                nc.scalar.copy(out=turned[:], in_=turned_ps[:])
+                tiles["turned", piece, j] = turned
+
+            def pool(piece, j):
+                if j == 0:
+                    for i in range(M // 2):
+                        tiles["pooled", piece, i] = psum_pooled.tile(
+                            [P, 2, PACK, 2, HALVES, POOLED], F32, name="pooled%d" % i, tag="pooled"
+                        )
+                for m in range(M):
+                    for h in range(HALVES):
+                        nc.tensor.matmul(
+                            out=tiles["pooled", piece, m // 2][:, :, j, m % 2, h, :],
+                            lhsT=tiles["turned", piece, j][:, m, h, :],
+                            rhs=pool_mat[:],
+                            start=True,
+                            stop=True,
+                        )
+
+            def round_means(piece):
                 grouped_tr = once.tile([P, 2, SMALL, PACK], BF16, align_bytes=64, name="grouped_tr")
                 for i in range(M // 2):
                     nc.scalar.copy(
                         out=grouped_tr[:, :, i * (SMALL // 2) : (i + 1) * (SMALL // 2), :],
-                        in_=pooled[i][:].rearrange("p s j m h x -> p s (m h x) j"),
+                        in_=tiles["pooled", piece, i][:].rearrange("p s j m h x -> p s (m h x) j"),
                     )
-                grouped_am = once.tile([P, RUN, PACK], BF16, align_bytes=64, name="grouped_am")
-                nc.scalar.activation(
-                    out=grouped_am[:].rearrange("p (t x) j -> p t x j", t=NT),
-                    in_=m_sums[:].rearrange("p j (x t) -> p t x j", t=NT),
-                    func=ACT.Copy,
-                    scale=1.0 / M,
-                )
-                return {"a": (a_codes, a_scales), "grouped_am": grouped_am, "grouped_tr": grouped_tr}
+                tiles["grouped_tr", piece] = grouped_tr
 
-            def back(ops):
+            def quantise_means(piece):
                 am_codes = twice.tile([P, RUN], U32, align_bytes=64, name="am_codes")
                 am_scales = twice.tile([P, RUN], U8, align_bytes=64, name="am_scales")
                 nc.vector.quantize_mx(
                     out=am_codes[:].bitcast(FP8X4),
                     scales=am_scales[:],
-                    in_=ops["grouped_am"][:].rearrange("p w j -> p (w j)"),
+                    in_=tiles["grouped_am", piece][:].rearrange("p w j -> p (w j)"),
                 )
                 tr_codes = twice.tile([P, 2 * SMALL], U32, align_bytes=64, name="tr_codes")
                 nc.vector.quantize_mx(
                     out=tr_codes[:].bitcast(FP8X4),
                     scales=tr_scales[:],
-                    in_=ops["grouped_tr"][:].rearrange("p s w j -> p (s w j)"),
+                    in_=tiles["grouped_tr", piece][:].rearrange("p s w j -> p (s w j)"),
                 )
                 at_rep_codes = twice.tile([P, COLS], U32, align_bytes=64, name="at_rep_codes")
                 at_rep_scales = twice.tile([P, COLS], U8, align_bytes=64, name="at_rep_scales")
@@ -249,16 +261,14 @@ def tile_layer_3d_dep_pa_t_kernel(tc, A, P1, P2, P3, P4, a5, gamma, beta, out):
                     .unsqueeze(2)
                     .to_broadcast([P, M, NT, KR // 4]),
                 )
-                ops["am"] = (am_codes, am_scales)
-                ops["at_rep"] = (at_rep_codes, at_rep_scales)
-                ops["ar"] = (tr_codes[:, SMALL : 2 * SMALL], tr_scales[:, SMALL : 2 * SMALL])
+                tiles["am_codes", piece], tiles["am_scales", piece] = am_codes, am_scales
+                tiles["tr_codes", piece] = tr_codes
+                tiles["at_rep_codes", piece], tiles["at_rep_scales", piece] = at_rep_codes, at_rep_scales
 
-            def mixes(piece, ops):
+            def terms_without_r(piece):
                 b, kq = divmod(piece, PIECES_PER_B)
-                a_codes, a_scales = ops["a"]
-                am_codes, am_scales = ops["am"]
-                at_rep_codes, at_rep_scales = ops["at_rep"]
-                ar_codes, ar_scales = ops["ar"]
+                ar_codes = tiles["tr_codes", piece][:, SMALL : 2 * SMALL]
+                ar_scales = tr_scales[:, SMALL : 2 * SMALL]
                 a4_acc = psum_small.tile([P, O_TILES, SMALL], F32, tag="small", name="a4_acc")
                 no_r = twice.tile([P, O_TILES, M, K_PIECE, NT], F32, name="no_r")
                 for ot in range(O_TILES):
@@ -275,58 +285,75 @@ def tile_layer_3d_dep_pa_t_kernel(tc, A, P1, P2, P3, P4, a5, gamma, beta, out):
                         op0=ALU.mult,
                         op1=ALU.add,
                     )
+                tiles["no_r", piece] = no_r
 
-                for ot in range(O_TILES):
-                    for m0 in range(0, M, 2):
-                        acc = psum_x.tile([P, 2, RUN], F32, name="acc")
-                        for i in range(2):
-                            cols = slice((m0 + i) * RUN, (m0 + i + 1) * RUN)
-                            mix(acc[:, i, :], W_A1_HI, ot, a_codes[:, cols], a_scales[:, cols], True, False)
-                            mix(acc[:, i, :], W_A1_LO, ot, a_codes[:, cols], a_scales[:, cols], False, False)
-                            mix(acc[:, i, :], W_A2, ot, am_codes[:], am_scales[:], False, False)
-                            mix(
-                                acc[:, i, :], W_A3, ot, at_rep_codes[:, cols], at_rep_scales[:, cols],
-                                False, True,
-                            )
-                        for i in range(2):
-                            cols = slice((m0 + i) * RUN, (m0 + i + 1) * RUN)
-                            nc.vector.tensor_tensor(
-                                out=y[:, ot, piece, cols].rearrange("p (t k r) -> p t k r", t=NT, r=NR),
-                                in0=acc[:, i, :].rearrange("p (t k r) -> p t k r", t=NT, r=NR),
-                                in1=no_r[:, ot, m0 + i, :, :]
-                                .rearrange("p k t -> p t k")
-                                .unsqueeze(3)
-                                .to_broadcast([P, NT, K_PIECE, NR]),
-                                op=ALU.add,
-                            )
+            def mix_bank(piece, bank):
+                ot, m_pair = divmod(bank, M // 2)
+                acc = psum_x.tile([P, 2, RUN], F32, name="acc")
+                for i in range(2):
+                    cols = slice((2 * m_pair + i) * RUN, (2 * m_pair + i + 1) * RUN)
+                    a_codes, a_scales = tiles["a_codes", piece][:, cols], tiles["a_scales", piece][:, cols]
+                    mix(acc[:, i, :], W_A1_HI, ot, a_codes, a_scales, True, False)
+                    mix(acc[:, i, :], W_A1_LO, ot, a_codes, a_scales, False, False)
+                    mix(
+                        acc[:, i, :], W_A2, ot, tiles["am_codes", piece][:], tiles["am_scales", piece][:],
+                        False, False,
+                    )
+                    mix(
+                        acc[:, i, :], W_A3, ot, tiles["at_rep_codes", piece][:, cols],
+                        tiles["at_rep_scales", piece][:, cols], False, True,
+                    )
+                for i in range(2):
+                    cols = slice((2 * m_pair + i) * RUN, (2 * m_pair + i + 1) * RUN)
+                    nc.vector.tensor_tensor(
+                        out=y[:, ot, piece, cols].rearrange("p (t k r) -> p t k r", t=NT, r=NR),
+                        in0=acc[:, i, :].rearrange("p (t k r) -> p t k r", t=NT, r=NR),
+                        in1=tiles["no_r", piece][:, ot, 2 * m_pair + i, :, :]
+                        .rearrange("p k t -> p t k")
+                        .unsqueeze(3)
+                        .to_broadcast([P, NT, K_PIECE, NR]),
+                        op=ALU.add,
+                    )
 
-            def activate(piece):
-                for ot in range(O_TILES):
-                    y_piece = y[:, ot, piece, :]
+            def activate(piece, part):
+                ot, second = divmod(part, 2)
+                y_piece = y[:, ot, piece, :]
+                if not second:
                     nc.scalar.activation(
                         out=y_piece, in_=y_piece, func=ACT.Relu,
                         accum_out=sums[:, ot, piece : piece + 1],
                     )
+                else:
                     squared = twice.tile([P, COLS], BF16, name="squared")
                     nc.scalar.activation(
                         out=squared[:], in_=y_piece, func=ACT.Square,
                         accum_out=squares[:, ot, piece : piece + 1],
                     )
 
+            assert PACK == O_TILES * (M // 2)
             with tc.manual_schedule():
-                operands = {0: front(raws[0])}
-                back(operands[0])
-                for piece in range(N_PIECES):
-                    if piece + 2 < N_PIECES:
-                        raws[piece + 2] = load(piece + 2)
-                    if piece + 1 < N_PIECES:
-                        operands[piece + 1] = front(raws[piece + 1])
-                    if piece > 0:
-                        activate(piece - 1)
-                    mixes(piece, operands[piece])
-                    if piece + 1 < N_PIECES:
-                        back(operands[piece + 1])
-                activate(N_PIECES - 1)
+                for i in range(-1, N_PIECES + 1):
+                    ahead, here, behind = i + 1, i, i - 1
+                    prepares = ahead < N_PIECES
+                    multiplies = 0 <= here < N_PIECES
+                    if 2 <= ahead + 1 < N_PIECES:
+                        tiles["raw", ahead + 1] = load(ahead + 1)
+                    if prepares:
+                        prepare_a(ahead)
+                    if multiplies:
+                        terms_without_r(here)
+                    for s in range(PACK + 1):
+                        if prepares and s < PACK:
+                            turn(ahead, s)
+                        if behind >= 0 and s < PACK:
+                            activate(behind, s)
+                        if prepares and s > 0:
+                            pool(ahead, s - 1)
+                        if multiplies and s > 0:
+                            mix_bank(here, s - 1)
+                    if prepares:
+                        round_means(ahead)
+                        quantise_means(ahead)
 
         count = float(B * POSITIONS)
         mean = keep.tile([P, O_TILES], F32)
@@ -358,18 +385,20 @@ def tile_layer_3d_dep_pa_t_kernel(tc, A, P1, P2, P3, P4, a5, gamma, beta, out):
                 for m in range(M):
                     source = y[
                         :, ot, b * PIECES_PER_B : (b + 1) * PIECES_PER_B, m * RUN : (m + 1) * RUN
-                    ].rearrange("p q (t x) -> p q x t", t=NT)
+                    ].rearrange("p q (th tl x) -> p th q x tl", tl=T_RUN, x=KR)
                     staged = staged_pool.tile([P, PIECES_PER_B, KR, NT], F32)
-                    if step % 2 == 0:
-                        nc.vector.tensor_scalar(
-                            out=staged[:], in0=source, scalar1=gain[:, ot : ot + 1],
-                            scalar2=shift[:, ot : ot + 1], op0=ALU.mult, op1=ALU.add,
-                        )
-                    else:
-                        nc.scalar.activation(
-                            out=staged[:], in_=source, func=ACT.Identity,
-                            bias=shift[:, ot : ot + 1], scale=gain[:, ot : ot + 1],
-                        )
+                    target = staged[:].rearrange("p q x (th tl) -> p th q x tl", tl=T_RUN)
+                    for th in range(NT // T_RUN):
+                        if step % 2 == 0:
+                            nc.vector.tensor_scalar(
+                                out=target[:, th], in0=source[:, th], scalar1=gain[:, ot : ot + 1],
+                                scalar2=shift[:, ot : ot + 1], op0=ALU.mult, op1=ALU.add,
+                            )
+                        else:
+                            nc.scalar.activation(
+                                out=target[:, th], in_=source[:, th], func=ACT.Identity,
+                                bias=shift[:, ot : ot + 1], scale=gain[:, ot : ot + 1],
+                            )
                     nc.sync.dma_start(
                         out=out_b[:, ot, m, :], in_=staged[:].rearrange("p q x t -> p (q x t)")
                     )

@@ -29,7 +29,7 @@ COLS = M * RUN
 SMALL = M * KR
 HALVES = RUN // P
 K_SQUARE = K_PIECE // HALVES
-T_RUN = 4
+T_RUN = NT // 2
 POOLED = K_SQUARE * NR
 
 UP = 10.0
@@ -160,17 +160,16 @@ def tile_layer_3d_dep_pa_t_kernel(tc, A, P1, P2, P3, P4, a5, gamma, beta, out):
             def prepare_a(piece):
                 raw = tiles["raw", piece]
                 grouped_a = once.tile([P, COLS, PACK], BF16, align_bytes=64, name="grouped_a")
-                for th in range(NT // T_RUN):
-                    nc.vector.tensor_copy(
-                        out=grouped_a[:].rearrange(
-                            "p (m th tl x) j -> p th m x j tl", m=M, tl=T_RUN, x=KR
-                        )[:, th],
-                        in_=raw[:].rearrange("p j m (x th tl) -> p th m x j tl", x=KR, tl=T_RUN)[:, th],
-                    )
+                target = grouped_a[:].rearrange("p (m th tl x) j -> p th m x j tl", m=M, tl=T_RUN, x=KR)
+                source = raw[:].rearrange("p j m (x th tl) -> p th m x j tl", x=KR, tl=T_RUN)
+                for m in range(M // 2, M):
+                    nc.scalar.copy(out=target[:, 1, m], in_=source[:, 1, m])
+                nc.vector.tensor_copy(out=target[:, 0], in_=source[:, 0])
+                nc.vector.tensor_copy(out=target[:, 1, 0 : M // 2], in_=source[:, 1, 0 : M // 2])
                 pair_sums = once.tile([P, PACK, 2, RUN], F32, name="pair_sums")
                 nc.vector.tensor_add(out=pair_sums[:], in0=raw[:, :, 0:2, :], in1=raw[:, :, 2:4, :])
                 m_sums = once.tile([P, PACK, RUN], F32, name="m_sums")
-                nc.vector.tensor_add(
+                nc.gpsimd.tensor_add(
                     out=m_sums[:], in0=pair_sums[:, :, 0, :], in1=pair_sums[:, :, 1, :]
                 )
                 a_codes = twice.tile([P, COLS], U32, align_bytes=64, name="a_codes")
@@ -230,13 +229,6 @@ def tile_layer_3d_dep_pa_t_kernel(tc, A, P1, P2, P3, P4, a5, gamma, beta, out):
                 tiles["grouped_tr", piece] = grouped_tr
 
             def quantise_means(piece):
-                am_codes = twice.tile([P, RUN], U32, align_bytes=64, name="am_codes")
-                am_scales = twice.tile([P, RUN], U8, align_bytes=64, name="am_scales")
-                nc.vector.quantize_mx(
-                    out=am_codes[:].bitcast(FP8X4),
-                    scales=am_scales[:],
-                    in_=tiles["grouped_am", piece][:].rearrange("p w j -> p (w j)"),
-                )
                 tr_codes = twice.tile([P, 2 * SMALL], U32, align_bytes=64, name="tr_codes")
                 nc.vector.quantize_mx(
                     out=tr_codes[:].bitcast(FP8X4),
@@ -260,6 +252,13 @@ def tile_layer_3d_dep_pa_t_kernel(tc, A, P1, P2, P3, P4, a5, gamma, beta, out):
                     .rearrange("p (m x) -> p m x", m=M)
                     .unsqueeze(2)
                     .to_broadcast([P, M, NT, KR // 4]),
+                )
+                am_codes = twice.tile([P, RUN], U32, align_bytes=64, name="am_codes")
+                am_scales = twice.tile([P, RUN], U8, align_bytes=64, name="am_scales")
+                nc.vector.quantize_mx(
+                    out=am_codes[:].bitcast(FP8X4),
+                    scales=am_scales[:],
+                    in_=tiles["grouped_am", piece][:].rearrange("p w j -> p (w j)"),
                 )
                 tiles["am_codes", piece], tiles["am_scales", piece] = am_codes, am_scales
                 tiles["tr_codes", piece] = tr_codes

@@ -33,7 +33,7 @@ T_RUN = NT // 2
 POOLED = K_SQUARE * NR
 
 UP = 10.0
-STATIONARY = (("p1", 8.0), ("p1", 2.0), ("p2", 1.0), ("p3", 1.0), ("p4", 4.0), ("p4", 1.0))
+STATIONARY = (("p1", 8.0), ("p1", 2.0), ("p2", 1.0 / M), ("p3", 1.0), ("p4", 4.0), ("p4", 1.0))
 W_A1_HI, W_A1_LO, W_A2, W_A3, W_A4_HI, W_A4_LO = 0, 1, 2, 3, 4, 5
 
 FLOPS = 2 * O * C * B * POSITIONS * (8 + 2 + 1 + 1) // 8
@@ -157,7 +157,7 @@ def tile_layer_3d_dep_pa_t_kernel(tc, A, P1, P2, P3, P4, a5, gamma, beta, out):
 
             tiles = {("raw", 0): first_raws[0], ("raw", 1): first_raws[1]}
 
-            def prepare_a(piece):
+            def regroup_a(piece):
                 raw = tiles["raw", piece]
                 grouped_a = once.tile([P, COLS, PACK], BF16, align_bytes=64, name="grouped_a")
                 target = grouped_a[:].rearrange("p (m th tl x) j -> p th m x j tl", m=M, tl=T_RUN, x=KR)
@@ -166,28 +166,21 @@ def tile_layer_3d_dep_pa_t_kernel(tc, A, P1, P2, P3, P4, a5, gamma, beta, out):
                     nc.scalar.copy(out=target[:, 1, m], in_=source[:, 1, m])
                 nc.vector.tensor_copy(out=target[:, 0], in_=source[:, 0])
                 nc.vector.tensor_copy(out=target[:, 1, 0 : M // 2], in_=source[:, 1, 0 : M // 2])
-                pair_sums = once.tile([P, PACK, 2, RUN], F32, name="pair_sums")
-                nc.vector.tensor_add(out=pair_sums[:], in0=raw[:, :, 0:2, :], in1=raw[:, :, 2:4, :])
-                m_sums = once.tile([P, PACK, RUN], F32, name="m_sums")
-                nc.gpsimd.tensor_add(
-                    out=m_sums[:], in0=pair_sums[:, :, 0, :], in1=pair_sums[:, :, 1, :]
-                )
+                tiles["grouped_a", piece] = grouped_a
+
+            def quantise_a(piece):
+                by_m = tiles["grouped_a", piece][:].rearrange("p (m w) j -> p m (w j)", m=M)
+                pair_sums = once.tile([P, 2, RUN * PACK], F32, name="pair_sums")
+                nc.vector.tensor_add(out=pair_sums[:], in0=by_m[:, 0:2, :], in1=by_m[:, 2:4, :])
                 a_codes = twice.tile([P, COLS], U32, align_bytes=64, name="a_codes")
                 a_scales = twice.tile([P, COLS], U8, align_bytes=64, name="a_scales")
                 nc.vector.quantize_mx(
                     out=a_codes[:].bitcast(FP8X4),
                     scales=a_scales[:],
-                    in_=grouped_a[:].rearrange("p w j -> p (w j)"),
+                    in_=tiles["grouped_a", piece][:].rearrange("p w j -> p (w j)"),
                 )
-                grouped_am = once.tile([P, RUN, PACK], BF16, align_bytes=64, name="grouped_am")
-                nc.gpsimd.tensor_scalar(
-                    out=grouped_am[:].rearrange("p (t x) j -> p t x j", t=NT),
-                    in0=m_sums[:].rearrange("p j (x t) -> p t x j", t=NT),
-                    scalar1=1.0 / M,
-                    scalar2=0.0,
-                    op0=ALU.mult,
-                    op1=ALU.add,
-                )
+                grouped_am = once.tile([P, RUN * PACK], BF16, align_bytes=64, name="grouped_am")
+                nc.vector.tensor_add(out=grouped_am[:], in0=pair_sums[:, 0, :], in1=pair_sums[:, 1, :])
                 tiles["grouped_am", piece] = grouped_am
                 tiles["a_codes", piece], tiles["a_scales", piece] = a_codes, a_scales
 
@@ -258,7 +251,7 @@ def tile_layer_3d_dep_pa_t_kernel(tc, A, P1, P2, P3, P4, a5, gamma, beta, out):
                 nc.vector.quantize_mx(
                     out=am_codes[:].bitcast(FP8X4),
                     scales=am_scales[:],
-                    in_=tiles["grouped_am", piece][:].rearrange("p w j -> p (w j)"),
+                    in_=tiles["grouped_am", piece][:],
                 )
                 tiles["am_codes", piece], tiles["am_scales", piece] = am_codes, am_scales
                 tiles["tr_codes", piece] = tr_codes
@@ -338,9 +331,11 @@ def tile_layer_3d_dep_pa_t_kernel(tc, A, P1, P2, P3, P4, a5, gamma, beta, out):
                     if 2 <= ahead + 1 < N_PIECES:
                         tiles["raw", ahead + 1] = load(ahead + 1)
                     if prepares:
-                        prepare_a(ahead)
+                        regroup_a(ahead)
                     if multiplies:
                         terms_without_r(here)
+                    if prepares:
+                        quantise_a(ahead)
                     for s in range(PACK + 1):
                         if prepares and s < PACK:
                             turn(ahead, s)

@@ -31,6 +31,7 @@ HALVES = RUN // P
 K_SQUARE = K_PIECE // HALVES
 T_RUN = NT // 2
 POOLED = K_SQUARE * NR
+SMALL_COLS = 2 * SMALL + RUN
 
 UP = 10.0
 STATIONARY = (("p1", 8.0), ("p1", 2.0), ("p2", 1.0 / M), ("p3", 1.0), ("p4", 4.0), ("p4", 1.0))
@@ -57,8 +58,12 @@ def tile_layer_3d_dep_pa_t_kernel(tc, A, P1, P2, P3, P4, a5, gamma, beta, out):
         y = keep.tile([P, O_TILES, N_PIECES, COLS], F32)
         sums = keep.tile([P, O_TILES, N_PIECES], F32)
         squares = keep.tile([P, O_TILES, N_PIECES], F32)
-        tr_scales = keep.tile([P, 2 * SMALL], U8, align_bytes=64)
-        nc.vector.memset(tr_scales[:].bitcast(I32), 0)
+        small_scales = [
+            keep.tile([P, SMALL_COLS], U8, align_bytes=64, name="small_scales%d" % parity)
+            for parity in range(2)
+        ]
+        for parity in range(2):
+            nc.vector.memset(small_scales[parity][:].bitcast(I32), 0)
         ident_bf16 = keep.tile([P, P], BF16)
         make_identity(nc, ident_bf16[:])
         pool_mat = keep.tile([P, 2, POOLED], BF16)
@@ -179,9 +184,11 @@ def tile_layer_3d_dep_pa_t_kernel(tc, A, P1, P2, P3, P4, a5, gamma, beta, out):
                     scales=a_scales[:],
                     in_=tiles["grouped_a", piece][:].rearrange("p w j -> p (w j)"),
                 )
-                grouped_am = once.tile([P, RUN * PACK], BF16, align_bytes=64, name="grouped_am")
-                nc.vector.tensor_add(out=grouped_am[:], in0=pair_sums[:, 0, :], in1=pair_sums[:, 1, :])
-                tiles["grouped_am", piece] = grouped_am
+                grouped_small = once.tile([P, SMALL_COLS * PACK], BF16, align_bytes=64, name="grouped_small")
+                nc.vector.tensor_add(
+                    out=grouped_small[:, 2 * SMALL * PACK :], in0=pair_sums[:, 0, :], in1=pair_sums[:, 1, :]
+                )
+                tiles["grouped_small", piece] = grouped_small
                 tiles["a_codes", piece], tiles["a_scales", piece] = a_codes, a_scales
 
             def turn(piece, j):
@@ -213,26 +220,26 @@ def tile_layer_3d_dep_pa_t_kernel(tc, A, P1, P2, P3, P4, a5, gamma, beta, out):
                         )
 
             def round_means(piece):
-                grouped_tr = once.tile([P, 2, SMALL, PACK], BF16, align_bytes=64, name="grouped_tr")
+                grouped_tr = tiles["grouped_small", piece][:, 0 : 2 * SMALL * PACK].rearrange(
+                    "p (s w j) -> p s w j", s=2, j=PACK
+                )
                 for i in range(M // 2):
                     nc.scalar.copy(
                         out=grouped_tr[:, :, i * (SMALL // 2) : (i + 1) * (SMALL // 2), :],
                         in_=tiles["pooled", piece, i][:].rearrange("p s j m h x -> p s (m h x) j"),
                     )
-                tiles["grouped_tr", piece] = grouped_tr
 
             def quantise_means(piece):
-                tr_codes = twice.tile([P, 2 * SMALL], U32, align_bytes=64, name="tr_codes")
+                small_codes = twice.tile([P, SMALL_COLS], U32, align_bytes=64, name="small_codes")
+                scales = small_scales[piece % 2]
                 nc.vector.quantize_mx(
-                    out=tr_codes[:].bitcast(FP8X4),
-                    scales=tr_scales[:],
-                    in_=tiles["grouped_tr", piece][:].rearrange("p s w j -> p (s w j)"),
+                    out=small_codes[:].bitcast(FP8X4), scales=scales[:], in_=tiles["grouped_small", piece][:]
                 )
                 at_rep_codes = twice.tile([P, COLS], U32, align_bytes=64, name="at_rep_codes")
                 at_rep_scales = twice.tile([P, COLS], U8, align_bytes=64, name="at_rep_scales")
                 nc.vector.tensor_copy(
                     out=at_rep_codes[:].bitcast(I32).rearrange("p (m t x) -> p m t x", m=M, t=NT),
-                    in_=tr_codes[:, 0:SMALL]
+                    in_=small_codes[:, 0:SMALL]
                     .bitcast(I32)
                     .rearrange("p (m x) -> p m x", m=M)
                     .unsqueeze(2)
@@ -240,72 +247,77 @@ def tile_layer_3d_dep_pa_t_kernel(tc, A, P1, P2, P3, P4, a5, gamma, beta, out):
                 )
                 nc.vector.tensor_copy(
                     out=at_rep_scales[:].bitcast(I32).rearrange("p (m t x) -> p m t x", m=M, t=NT),
-                    in_=tr_scales[:, 0:SMALL]
+                    in_=scales[:, 0:SMALL]
                     .bitcast(I32)
                     .rearrange("p (m x) -> p m x", m=M)
                     .unsqueeze(2)
                     .to_broadcast([P, M, NT, KR // 4]),
                 )
-                am_codes = twice.tile([P, RUN], U32, align_bytes=64, name="am_codes")
-                am_scales = twice.tile([P, RUN], U8, align_bytes=64, name="am_scales")
-                nc.vector.quantize_mx(
-                    out=am_codes[:].bitcast(FP8X4),
-                    scales=am_scales[:],
-                    in_=tiles["grouped_am", piece][:],
-                )
-                tiles["am_codes", piece], tiles["am_scales", piece] = am_codes, am_scales
-                tiles["tr_codes", piece] = tr_codes
+                tiles["small_codes", piece] = small_codes
                 tiles["at_rep_codes", piece], tiles["at_rep_scales", piece] = at_rep_codes, at_rep_scales
 
-            def terms_without_r(piece):
+            def scale_a5(piece):
                 b, kq = divmod(piece, PIECES_PER_B)
-                ar_codes = tiles["tr_codes", piece][:, SMALL : 2 * SMALL]
-                ar_scales = tr_scales[:, SMALL : 2 * SMALL]
-                a4_acc = psum_small.tile([P, O_TILES, SMALL], F32, tag="small", name="a4_acc")
-                no_r = twice.tile([P, O_TILES, M, K_PIECE, NT], F32, name="no_r")
+                a5_of_b = a5_sb[:].rearrange("p g x -> p (g x)")[
+                    :, b * O_TILES * M * K * NT : (b + 1) * O_TILES * M * K * NT
+                ]
+                a5_scaled = twice.tile([P, O_TILES * M, NT * K_PIECE], F32, name="a5_scaled")
+                nc.gpsimd.tensor_scalar(
+                    out=a5_scaled[:].rearrange("p g (t k) -> p g t k", t=NT),
+                    in0=a5_of_b.rearrange(
+                        "p (g kq k t) -> p kq g t k", kq=PIECES_PER_B, k=K_PIECE, t=NT
+                    )[:, kq],
+                    scalar1=2.0 * UP,
+                    scalar2=0.0,
+                    op0=ALU.mult,
+                    op1=ALU.add,
+                )
+                tiles["a5_scaled", piece] = a5_scaled
+
+            def terms_without_r(piece):
+                ar_codes = tiles["small_codes", piece][:, SMALL : 2 * SMALL]
+                ar_scales = small_scales[piece % 2][:, SMALL : 2 * SMALL]
+                a4_acc = psum_small.tile([P, O_TILES * SMALL], F32, tag="small", name="a4_acc")
                 for ot in range(O_TILES):
-                    mix(a4_acc[:, ot, :], W_A4_HI, ot, ar_codes, ar_scales, True, False)
-                    mix(a4_acc[:, ot, :], W_A4_LO, ot, ar_codes, ar_scales, False, True)
-                for ot in range(O_TILES):
-                    nc.vector.scalar_tensor_tensor(
-                        out=no_r[:, ot].rearrange("p m k t -> p m (k t)"),
-                        in0=a5_sb[:, b * O_TILES + ot, :].rearrange(
-                            "p (m kq x) -> p m kq x", m=M, kq=PIECES_PER_B
-                        )[:, :, kq, :],
-                        scalar=2.0 * UP,
-                        in1=a4_acc[:, ot, :].rearrange("p (m x) -> p m x", m=M),
-                        op0=ALU.mult,
-                        op1=ALU.add,
-                    )
+                    a4_cols = a4_acc[:, ot * SMALL : (ot + 1) * SMALL]
+                    mix(a4_cols, W_A4_HI, ot, ar_codes, ar_scales, True, False)
+                    mix(a4_cols, W_A4_LO, ot, ar_codes, ar_scales, False, True)
+                no_r = twice.tile([P, O_TILES * M, NT * K_PIECE], F32, name="no_r")
+                nc.vector.tensor_tensor(
+                    out=no_r[:].rearrange("p g (t k) -> p g t k", t=NT),
+                    in0=a4_acc[:].rearrange("p (g k t) -> p g t k", k=K_PIECE, t=NT),
+                    in1=tiles["a5_scaled", piece][:].rearrange("p g (t k) -> p g t k", t=NT),
+                    op=ALU.add,
+                )
                 tiles["no_r", piece] = no_r
 
             def mix_bank(piece, bank):
                 ot, m_pair = divmod(bank, M // 2)
                 acc = psum_x.tile([P, 2, RUN], F32, name="acc")
+                am_codes = tiles["small_codes", piece][:, 2 * SMALL :]
+                am_scales = small_scales[piece % 2][:, 2 * SMALL :]
                 for i in range(2):
                     cols = slice((2 * m_pair + i) * RUN, (2 * m_pair + i + 1) * RUN)
                     a_codes, a_scales = tiles["a_codes", piece][:, cols], tiles["a_scales", piece][:, cols]
                     mix(acc[:, i, :], W_A1_HI, ot, a_codes, a_scales, True, False)
                     mix(acc[:, i, :], W_A1_LO, ot, a_codes, a_scales, False, False)
-                    mix(
-                        acc[:, i, :], W_A2, ot, tiles["am_codes", piece][:], tiles["am_scales", piece][:],
-                        False, False,
-                    )
+                    mix(acc[:, i, :], W_A2, ot, am_codes, am_scales, False, False)
                     mix(
                         acc[:, i, :], W_A3, ot, tiles["at_rep_codes", piece][:, cols],
                         tiles["at_rep_scales", piece][:, cols], False, True,
                     )
-                for i in range(2):
-                    cols = slice((2 * m_pair + i) * RUN, (2 * m_pair + i + 1) * RUN)
-                    nc.vector.tensor_tensor(
-                        out=y[:, ot, piece, cols].rearrange("p (t k r) -> p t k r", t=NT, r=NR),
-                        in0=acc[:, i, :].rearrange("p (t k r) -> p t k r", t=NT, r=NR),
-                        in1=tiles["no_r", piece][:, ot, 2 * m_pair + i, :, :]
-                        .rearrange("p k t -> p t k")
-                        .unsqueeze(3)
-                        .to_broadcast([P, NT, K_PIECE, NR]),
-                        op=ALU.add,
-                    )
+                g = ot * M + 2 * m_pair
+                nc.vector.tensor_tensor(
+                    out=y[:, ot, piece, 2 * m_pair * RUN : (2 * m_pair + 2) * RUN].rearrange(
+                        "p (x r) -> p x r", r=NR
+                    ),
+                    in0=acc[:].rearrange("p i (x r) -> p (i x) r", r=NR),
+                    in1=tiles["no_r", piece][:, g : g + 2, :]
+                    .rearrange("p g x -> p (g x)")
+                    .unsqueeze(2)
+                    .to_broadcast([P, 2 * NT * K_PIECE, NR]),
+                    op=ALU.add,
+                )
 
             def activate(piece, part):
                 ot, second = divmod(part, 2)
@@ -331,6 +343,7 @@ def tile_layer_3d_dep_pa_t_kernel(tc, A, P1, P2, P3, P4, a5, gamma, beta, out):
                     if 2 <= ahead + 1 < N_PIECES:
                         tiles["raw", ahead + 1] = load(ahead + 1)
                     if prepares:
+                        scale_a5(ahead)
                         regroup_a(ahead)
                     if multiplies:
                         terms_without_r(here)

@@ -162,21 +162,29 @@ def tile_layer_3d_dep_pa_t_kernel(tc, A, P1, P2, P3, P4, a5, gamma, beta, out):
 
             tiles = {("raw", 0): first_raws[0], ("raw", 1): first_raws[1]}
 
-            def regroup_a(piece):
+            def regroup_a_scalar(piece):
                 raw = tiles["raw", piece]
                 grouped_a = once.tile([P, COLS, PACK], BF16, align_bytes=64, name="grouped_a")
                 target = grouped_a[:].rearrange("p (m th tl x) j -> p th m x j tl", m=M, tl=T_RUN, x=KR)
                 source = raw[:].rearrange("p j m (x th tl) -> p th m x j tl", x=KR, tl=T_RUN)
                 for m in range(M // 2, M):
                     nc.scalar.copy(out=target[:, 1, m], in_=source[:, 1, m])
+                tiles["grouped_a", piece] = grouped_a
+                tiles["regroup_views", piece] = (target, source)
+
+            def regroup_a_vector(piece):
+                target, source = tiles["regroup_views", piece]
                 nc.vector.tensor_copy(out=target[:, 0], in_=source[:, 0])
                 nc.vector.tensor_copy(out=target[:, 1, 0 : M // 2], in_=source[:, 1, 0 : M // 2])
-                tiles["grouped_a", piece] = grouped_a
 
-            def quantise_a(piece):
+            def sum_pairs_of_m(piece):
                 by_m = tiles["grouped_a", piece][:].rearrange("p (m w) j -> p m (w j)", m=M)
                 pair_sums = once.tile([P, 2, RUN * PACK], F32, name="pair_sums")
                 nc.vector.tensor_add(out=pair_sums[:], in0=by_m[:, 0:2, :], in1=by_m[:, 2:4, :])
+                tiles["pair_sums", piece] = pair_sums
+
+            def quantise_a(piece):
+                pair_sums = tiles["pair_sums", piece]
                 a_codes = twice.tile([P, COLS], U32, align_bytes=64, name="a_codes")
                 a_scales = twice.tile([P, COLS], U8, align_bytes=64, name="a_scales")
                 nc.vector.quantize_mx(
@@ -306,6 +314,11 @@ def tile_layer_3d_dep_pa_t_kernel(tc, A, P1, P2, P3, P4, a5, gamma, beta, out):
                         acc[:, i, :], W_A3, ot, tiles["at_rep_codes", piece][:, cols],
                         tiles["at_rep_scales", piece][:, cols], False, True,
                     )
+                tiles["acc", piece, bank] = acc
+
+            def add_out(piece, bank):
+                ot, m_pair = divmod(bank, M // 2)
+                acc = tiles["acc", piece, bank]
                 g = ot * M + 2 * m_pair
                 nc.vector.tensor_tensor(
                     out=y[:, ot, piece, 2 * m_pair * RUN : (2 * m_pair + 2) * RUN].rearrange(
@@ -335,32 +348,51 @@ def tile_layer_3d_dep_pa_t_kernel(tc, A, P1, P2, P3, P4, a5, gamma, beta, out):
                     )
 
             assert PACK == O_TILES * (M // 2)
+            LAST = PACK - 1
             with tc.manual_schedule():
+                turn(0, 0)
                 for i in range(-1, N_PIECES + 1):
                     ahead, here, behind = i + 1, i, i - 1
                     prepares = ahead < N_PIECES
                     multiplies = 0 <= here < N_PIECES
+                    finishes = 0 <= behind < N_PIECES
                     if 2 <= ahead + 1 < N_PIECES:
                         tiles["raw", ahead + 1] = load(ahead + 1)
+                    if multiplies:
+                        quantise_means(here)
+                    if finishes:
+                        add_out(behind, LAST)
                     if prepares:
                         scale_a5(ahead)
-                        regroup_a(ahead)
-                    if multiplies:
-                        terms_without_r(here)
-                    if prepares:
-                        quantise_a(ahead)
-                    for s in range(PACK + 1):
-                        if prepares and s < PACK:
-                            turn(ahead, s)
-                        if behind >= 0 and s < PACK:
-                            activate(behind, s)
-                        if prepares and s > 0:
-                            pool(ahead, s - 1)
-                        if multiplies and s > 0:
-                            mix_bank(here, s - 1)
-                    if prepares:
-                        round_means(ahead)
-                        quantise_means(ahead)
+                        regroup_a_scalar(ahead)
+                    for unit in range(PACK):
+                        if prepares and unit < LAST:
+                            turn(ahead, unit + 1)
+                        if prepares:
+                            pool(ahead, unit)
+                        if prepares and unit == LAST:
+                            round_means(ahead)
+                            if ahead + 1 < N_PIECES:
+                                turn(ahead + 1, 0)
+                        if unit == 0:
+                            if multiplies:
+                                terms_without_r(here)
+                            if prepares:
+                                regroup_a_vector(ahead)
+                        if prepares and unit == 1:
+                            sum_pairs_of_m(ahead)
+                        if prepares and unit == 2:
+                            quantise_a(ahead)
+                        if multiplies:
+                            mix_bank(here, unit)
+                            if unit < LAST:
+                                add_out(here, unit)
+                        if finishes:
+                            if unit == 0:
+                                activate(behind, 0)
+                                activate(behind, 1)
+                            elif unit < LAST:
+                                activate(behind, unit + 1)
 
         count = float(B * POSITIONS)
         mean = keep.tile([P, O_TILES], F32)

@@ -208,7 +208,10 @@ def tile_layer_3d_dep_pa_t_kernel(tc, A, P1, P2, P3, P4, a5, gamma, beta, out):
                             turned_ps[:, m, h, :], raw[:, j, m, h * P : (h + 1) * P], ident_bf16[:]
                         )
                 turned = twice.tile([P, M, HALVES, P], BF16, name="turned")
-                nc.scalar.copy(out=turned[:], in_=turned_ps[:])
+                nc.scalar.copy(
+                    out=turned[:].rearrange("p m h c -> p (m h c)").bitcast(F32),
+                    in_=turned_ps[:].rearrange("p m h c -> p (m h c)").bitcast(F32),
+                )
                 tiles["turned", piece, j] = turned
 
             def pool(piece, j):

@@ -72,7 +72,7 @@ def tile_layer_3d_dep_pa_t_kernel(tc, A, P1, P2, P3, P4, a5, gamma, beta, out):
         nc.vector.memset(table_warmer[:], 1.0)
         nc.scalar.sqrt(out=table_warmer[:], in_=table_warmer[:])
 
-        raw_pool = ctx.enter_context(tc.tile_pool(name="raw_pool", bufs=2))
+        raw_pool = ctx.enter_context(tc.tile_pool(name="raw_pool", bufs=3))
 
         def load(piece):
             b, kq = divmod(piece, PIECES_PER_B)
@@ -146,6 +146,7 @@ def tile_layer_3d_dep_pa_t_kernel(tc, A, P1, P2, P3, P4, a5, gamma, beta, out):
         nc.sync.dma_start(
             out=a5_sb[:], in_=a5.rearrange("b (ot o) m k t -> o (b ot) (m k t)", o=P)
         )
+        first_raws[2] = load(2)
 
         with tc.tile_pool(name="once", bufs=1) as once, tc.tile_pool(name="twice", bufs=2) as twice:
 
@@ -160,7 +161,7 @@ def tile_layer_3d_dep_pa_t_kernel(tc, A, P1, P2, P3, P4, a5, gamma, beta, out):
                     stop=stop,
                 )
 
-            tiles = {("raw", 0): first_raws[0], ("raw", 1): first_raws[1]}
+            tiles = {("raw", piece): first_raws[piece] for piece in first_raws}
 
             def regroup_a_scalar(piece):
                 raw = tiles["raw", piece]
@@ -184,7 +185,6 @@ def tile_layer_3d_dep_pa_t_kernel(tc, A, P1, P2, P3, P4, a5, gamma, beta, out):
                 tiles["pair_sums", piece] = pair_sums
 
             def quantise_a(piece):
-                pair_sums = tiles["pair_sums", piece]
                 a_codes = twice.tile([P, COLS], U32, align_bytes=64, name="a_codes")
                 a_scales = twice.tile([P, COLS], U8, align_bytes=64, name="a_scales")
                 nc.vector.quantize_mx(
@@ -192,12 +192,15 @@ def tile_layer_3d_dep_pa_t_kernel(tc, A, P1, P2, P3, P4, a5, gamma, beta, out):
                     scales=a_scales[:],
                     in_=tiles["grouped_a", piece][:].rearrange("p w j -> p (w j)"),
                 )
+                tiles["a_codes", piece], tiles["a_scales", piece] = a_codes, a_scales
+
+            def finish_sum_over_m(piece):
+                pair_sums = tiles["pair_sums", piece]
                 grouped_small = once.tile([P, SMALL_COLS * PACK], BF16, align_bytes=64, name="grouped_small")
                 nc.vector.tensor_add(
                     out=grouped_small[:, 2 * SMALL * PACK :], in0=pair_sums[:, 0, :], in1=pair_sums[:, 1, :]
                 )
                 tiles["grouped_small", piece] = grouped_small
-                tiles["a_codes", piece], tiles["a_scales", piece] = a_codes, a_scales
 
             def turn(piece, j):
                 raw = tiles["raw", piece]
@@ -244,18 +247,22 @@ def tile_layer_3d_dep_pa_t_kernel(tc, A, P1, P2, P3, P4, a5, gamma, beta, out):
                 small_codes = twice.tile([P, SMALL_COLS], U32, align_bytes=64, name="small_codes")
                 scales = small_scales[piece % 2]
                 nc.vector.quantize_mx(
-                    out=small_codes[:].bitcast(FP8X4), scales=scales[:], in_=tiles["grouped_small", piece][:]
+                    out=small_codes[:, 0 : 2 * SMALL].bitcast(FP8X4),
+                    scales=scales[:, 0 : 2 * SMALL],
+                    in_=tiles["grouped_small", piece][:, 0 : 2 * SMALL * PACK],
                 )
                 at_rep_codes = twice.tile([P, COLS], U32, align_bytes=64, name="at_rep_codes")
                 at_rep_scales = twice.tile([P, COLS], U8, align_bytes=64, name="at_rep_scales")
-                nc.vector.tensor_copy(
-                    out=at_rep_codes[:].bitcast(I32).rearrange("p (m t x) -> p m t x", m=M, t=NT),
-                    in_=small_codes[:, 0:SMALL]
-                    .bitcast(I32)
-                    .rearrange("p (m x) -> p m x", m=M)
-                    .unsqueeze(2)
-                    .to_broadcast([P, M, NT, KR]),
-                )
+                for m in range(M):
+                    nc.sync.dma_start(
+                        out=at_rep_codes[:, m * RUN : (m + 1) * RUN]
+                        .bitcast(I32)
+                        .rearrange("p (t x) -> p t x", t=NT),
+                        in_=small_codes[:, m * KR : (m + 1) * KR]
+                        .bitcast(I32)
+                        .unsqueeze(1)
+                        .to_broadcast([P, NT, KR]),
+                    )
                 nc.vector.tensor_copy(
                     out=at_rep_scales[:].bitcast(I32).rearrange("p (m t x) -> p m t x", m=M, t=NT),
                     in_=scales[:, 0:SMALL]
@@ -266,6 +273,13 @@ def tile_layer_3d_dep_pa_t_kernel(tc, A, P1, P2, P3, P4, a5, gamma, beta, out):
                 )
                 tiles["small_codes", piece] = small_codes
                 tiles["at_rep_codes", piece], tiles["at_rep_scales", piece] = at_rep_codes, at_rep_scales
+
+            def quantise_sum_over_m(piece):
+                nc.vector.quantize_mx(
+                    out=tiles["small_codes", piece][:, 2 * SMALL :].bitcast(FP8X4),
+                    scales=small_scales[piece % 2][:, 2 * SMALL :],
+                    in_=tiles["grouped_small", piece][:, 2 * SMALL * PACK :],
+                )
 
             def scale_a5(piece):
                 b, kq = divmod(piece, PIECES_PER_B)
@@ -354,48 +368,66 @@ def tile_layer_3d_dep_pa_t_kernel(tc, A, P1, P2, P3, P4, a5, gamma, beta, out):
             LAST = PACK - 1
             with tc.manual_schedule():
                 turn(0, 0)
+                turn(0, 1)
+                pool(0, 0)
                 for i in range(-1, N_PIECES + 1):
                     ahead, here, behind = i + 1, i, i - 1
                     prepares = ahead < N_PIECES
+                    turns_next = ahead + 1 < N_PIECES
                     multiplies = 0 <= here < N_PIECES
                     finishes = 0 <= behind < N_PIECES
-                    if 2 <= ahead + 1 < N_PIECES:
-                        tiles["raw", ahead + 1] = load(ahead + 1)
-                    if multiplies:
-                        quantise_means(here)
+                    if 3 <= ahead + 2 < N_PIECES:
+                        tiles["raw", ahead + 2] = load(ahead + 2)
                     if finishes:
                         add_out(behind, LAST)
                     if prepares:
                         scale_a5(ahead)
                         regroup_a_scalar(ahead)
-                    for unit in range(PACK):
-                        if prepares and unit < LAST:
-                            turn(ahead, unit + 1)
-                        if prepares:
-                            pool(ahead, unit)
-                        if prepares and unit == LAST:
-                            round_means(ahead)
-                            if ahead + 1 < N_PIECES:
-                                turn(ahead + 1, 0)
-                        if unit == 0:
-                            if multiplies:
-                                terms_without_r(here)
-                            if prepares:
-                                regroup_a_vector(ahead)
-                        if prepares and unit == 1:
-                            sum_pairs_of_m(ahead)
-                        if prepares and unit == 2:
-                            quantise_a(ahead)
-                        if multiplies:
-                            mix_bank(here, unit)
-                            if unit < LAST:
-                                add_out(here, unit)
-                        if finishes:
-                            if unit == 0:
-                                activate(behind, 0)
-                                activate(behind, 1)
-                            elif unit < LAST:
-                                activate(behind, unit + 1)
+                    if prepares:
+                        turn(ahead, 2)
+                        pool(ahead, 1)
+                    if multiplies:
+                        terms_without_r(here)
+                    if prepares:
+                        regroup_a_vector(ahead)
+                    if multiplies:
+                        mix_bank(here, 0)
+                        add_out(here, 0)
+                    if finishes:
+                        activate(behind, 0)
+                    if prepares:
+                        turn(ahead, 3)
+                        pool(ahead, 2)
+                        sum_pairs_of_m(ahead)
+                    if multiplies:
+                        mix_bank(here, 1)
+                        add_out(here, 1)
+                    if finishes:
+                        activate(behind, 1)
+                        activate(behind, 2)
+                    if prepares:
+                        pool(ahead, 3)
+                        finish_sum_over_m(ahead)
+                        round_means(ahead)
+                    if turns_next:
+                        turn(ahead + 1, 0)
+                    if prepares:
+                        quantise_means(ahead)
+                    if multiplies:
+                        mix_bank(here, 2)
+                    if prepares:
+                        quantise_a(ahead)
+                    if multiplies:
+                        add_out(here, 2)
+                    if finishes:
+                        activate(behind, 3)
+                    if turns_next:
+                        turn(ahead + 1, 1)
+                        pool(ahead + 1, 0)
+                    if prepares:
+                        quantise_sum_over_m(ahead)
+                    if multiplies:
+                        mix_bank(here, LAST)
 
         count = float(B * POSITIONS)
         mean = keep.tile([P, O_TILES], F32)

@@ -34,8 +34,8 @@ POOLED = K_SQUARE * NR
 SMALL_COLS = 2 * SMALL + RUN
 
 UP = 10.0
-STATIONARY = (("p1", 8.0), ("p1", 2.0), ("p2", 1.0 / M), ("p3", 1.0), ("p4", 4.0), ("p4", 1.0))
-W_A1_HI, W_A1_LO, W_A2, W_A3, W_A4_HI, W_A4_LO = 0, 1, 2, 3, 4, 5
+STATIONARY = (("p1", 8.0), ("p1", 2.0), ("p2", 1.0 / M), ("p3", 1.0), ("p4", 1.0))
+W_A1_HI, W_A1_LO, W_A2, W_A3, W_A4 = 0, 1, 2, 3, 4
 
 FLOPS = 2 * O * C * B * POSITIONS * (8 + 2 + 1 + 1) // 8
 
@@ -85,9 +85,11 @@ def tile_layer_3d_dep_pa_t_kernel(tc, A, P1, P2, P3, P4, a5, gamma, beta, out):
             )
             return raw
 
-        first_raws = {0: load(0)}
+        ctx.enter_context(tc.manual_schedule())
 
         with tc.tile_pool(name="setup", bufs=2) as setup:
+            gb_rows = setup.tile([P, P], BF16, tag="gb_rows")
+            nc.vector.memset(gb_rows[:], 0.0)
             ident_f32 = setup.tile([P, P], F32, tag="ident_f32")
             make_identity(nc, ident_f32[:])
 
@@ -107,46 +109,50 @@ def tile_layer_3d_dep_pa_t_kernel(tc, A, P1, P2, P3, P4, a5, gamma, beta, out):
             nc.vector.tensor_scalar_mul(out=pool_mat[:, 0, :], in0=pool_ones[:, 0, :], scalar1=1.0 / NT)
             nc.vector.tensor_scalar_mul(out=pool_mat[:, 1, :], in0=pool_ones[:, 1, :], scalar1=1.0 / NR)
 
-            grouped_w = {}
+            all_w_rows = {}
             for name in ("p1", "p2", "p3", "p4"):
-                w_rows = setup.tile([P, O_TILES, C], BF16, tag="w_rows")
+                w_rows = setup.tile([P, O_TILES, C], BF16, name="w_rows_" + name, bufs=1)
                 nc.sync.dma_start(
                     out=w_rows[:], in_=weights[name].rearrange("(ot o) c -> o ot c", o=P)
                 )
+                all_w_rows[name] = w_rows
+            nc.sync.dma_start(out=gb_rows[0:O_TILES, :], in_=gamma.rearrange("(ot o) -> ot o", o=P))
+            nc.sync.dma_start(
+                out=gb_rows[O_TILES : 2 * O_TILES, :], in_=beta.rearrange("(ot o) -> ot o", o=P)
+            )
+            first_raws = {0: load(0), 1: load(1)}
+            nc.sync.dma_start(
+                out=a5_sb[:], in_=a5.rearrange("b (ot o) m k t -> o (b ot) (m k t)", o=P)
+            )
+            first_raws[2] = load(2)
+
+            grouped_w = {}
+            for name in ("p1", "p2", "p3", "p4"):
+                w_rows = all_w_rows[name]
                 words = w_rows[:].bitcast(F32).rearrange("o ot (p u) -> o ot u p", u=2)
-                turned = psum_small.tile([P, O_TILES, 2, P], F32, tag="small")
+                turned = psum_x.tile([P, O_TILES, 2, P], F32, name="acc")
                 for ot in range(O_TILES):
                     for u in range(2):
                         nc.tensor.transpose(turned[:, ot, u, :], words[:, ot, u, :], ident_f32[:])
-                grouped = setup.tile([P, O * PACK], BF16, name="grouped_" + name, bufs=1)
-                nc.vector.tensor_copy(
+                grouped = setup.tile([P, O * PACK], BF16, name="grouped_" + name, bufs=1, align_bytes=64)
+                nc.scalar.copy(
                     out=grouped[:].bitcast(F32).rearrange("p (ot o u) -> p ot o u", ot=O_TILES, u=2),
                     in_=turned[:].rearrange("p ot u o -> p ot o u"),
                 )
                 grouped_w[name] = grouped
 
             for i, (name, factor) in enumerate(STATIONARY):
-                scaled = setup.tile([P, O * PACK], BF16, tag="scaled", align_bytes=64)
-                nc.vector.tensor_scalar_mul(out=scaled[:], in0=grouped_w[name][:], scalar1=factor)
+                scaled = grouped_w[name]
+                if factor != 1.0:
+                    scaled = setup.tile([P, O * PACK], BF16, tag="scaled", align_bytes=64)
+                    nc.vector.tensor_scalar_mul(out=scaled[:], in0=grouped_w[name][:], scalar1=factor)
                 nc.vector.quantize_mx(
                     out=w_codes[:, i, :].bitcast(FP8X4), scales=w_scales[:, i, :], in_=scaled[:]
                 )
 
-            gb_rows = setup.tile([P, P], BF16, tag="gb_rows")
-            nc.vector.memset(gb_rows[:], 0.0)
-            nc.sync.dma_start(out=gb_rows[0:O_TILES, :], in_=gamma.rearrange("(ot o) -> ot o", o=P))
-            nc.sync.dma_start(
-                out=gb_rows[O_TILES : 2 * O_TILES, :], in_=beta.rearrange("(ot o) -> ot o", o=P)
-            )
             gb_turned = psum_small.tile([P, P], BF16, tag="small")
             nc.tensor.transpose(gb_turned[:], gb_rows[:], ident_bf16[:])
             nc.vector.tensor_copy(out=gamma_beta[:], in_=gb_turned[:, 0 : 2 * O_TILES])
-
-        first_raws[1] = load(1)
-        nc.sync.dma_start(
-            out=a5_sb[:], in_=a5.rearrange("b (ot o) m k t -> o (b ot) (m k t)", o=P)
-        )
-        first_raws[2] = load(2)
 
         with tc.tile_pool(name="once", bufs=1) as once, tc.tile_pool(name="twice", bufs=2) as twice:
 
@@ -292,7 +298,7 @@ def tile_layer_3d_dep_pa_t_kernel(tc, A, P1, P2, P3, P4, a5, gamma, beta, out):
                     in0=a5_of_b.rearrange(
                         "p (g kq k t) -> p kq g t k", kq=PIECES_PER_B, k=K_PIECE, t=NT
                     )[:, kq],
-                    scalar1=2.0 * UP,
+                    scalar1=2.0 / 0.5,
                     scalar2=0.0,
                     op0=ALU.mult,
                     op1=ALU.add,
@@ -305,8 +311,7 @@ def tile_layer_3d_dep_pa_t_kernel(tc, A, P1, P2, P3, P4, a5, gamma, beta, out):
                 a4_acc = psum_small.tile([P, O_TILES * SMALL], F32, tag="small", name="a4_acc")
                 for ot in range(O_TILES):
                     a4_cols = a4_acc[:, ot * SMALL : (ot + 1) * SMALL]
-                    mix(a4_cols, W_A4_HI, ot, ar_codes, ar_scales, True, False)
-                    mix(a4_cols, W_A4_LO, ot, ar_codes, ar_scales, False, True)
+                    mix(a4_cols, W_A4, ot, ar_codes, ar_scales, True, True)
                 no_r = twice.tile([P, O_TILES * M, NT * K_PIECE], F32, name="no_r")
                 nc.vector.tensor_tensor(
                     out=no_r[:].rearrange("p g (t k) -> p g t k", t=NT),
@@ -337,16 +342,18 @@ def tile_layer_3d_dep_pa_t_kernel(tc, A, P1, P2, P3, P4, a5, gamma, beta, out):
                 ot, m_pair = divmod(bank, M // 2)
                 acc = tiles["acc", piece, bank]
                 g = ot * M + 2 * m_pair
-                nc.vector.tensor_tensor(
+                nc.vector.scalar_tensor_tensor(
                     out=y[:, ot, piece, 2 * m_pair * RUN : (2 * m_pair + 2) * RUN].rearrange(
                         "p (x r) -> p x r", r=NR
                     ),
-                    in0=acc[:].rearrange("p i (x r) -> p (i x) r", r=NR),
-                    in1=tiles["no_r", piece][:, g : g + 2, :]
+                    in0=tiles["no_r", piece][:, g : g + 2, :]
                     .rearrange("p g x -> p (g x)")
                     .unsqueeze(2)
                     .to_broadcast([P, 2 * NT * K_PIECE, NR]),
-                    op=ALU.add,
+                    scalar=0.5 * UP,
+                    in1=acc[:].rearrange("p i (x r) -> p (i x) r", r=NR),
+                    op0=ALU.mult,
+                    op1=ALU.add,
                 )
 
             def activate(piece, part):
@@ -366,114 +373,150 @@ def tile_layer_3d_dep_pa_t_kernel(tc, A, P1, P2, P3, P4, a5, gamma, beta, out):
 
             assert PACK == O_TILES * (M // 2)
             LAST = PACK - 1
-            with tc.manual_schedule():
-                turn(0, 0)
-                turn(0, 1)
-                pool(0, 0)
-                for i in range(-1, N_PIECES + 1):
-                    ahead, here, behind = i + 1, i, i - 1
-                    prepares = ahead < N_PIECES
-                    turns_next = ahead + 1 < N_PIECES
-                    multiplies = 0 <= here < N_PIECES
-                    finishes = 0 <= behind < N_PIECES
-                    if 3 <= ahead + 2 < N_PIECES:
-                        tiles["raw", ahead + 2] = load(ahead + 2)
-                    if finishes:
-                        add_out(behind, LAST)
-                    if prepares:
-                        scale_a5(ahead)
-                        regroup_a_scalar(ahead)
-                    if prepares:
-                        turn(ahead, 2)
-                        pool(ahead, 1)
-                    if multiplies:
-                        terms_without_r(here)
-                    if prepares:
-                        regroup_a_vector(ahead)
-                    if multiplies:
-                        mix_bank(here, 0)
-                        add_out(here, 0)
-                    if finishes:
-                        activate(behind, 0)
-                    if prepares:
-                        turn(ahead, 3)
-                        pool(ahead, 2)
-                        sum_pairs_of_m(ahead)
-                    if multiplies:
-                        mix_bank(here, 1)
-                        add_out(here, 1)
-                    if finishes:
-                        activate(behind, 1)
-                        activate(behind, 2)
-                    if prepares:
-                        pool(ahead, 3)
-                        finish_sum_over_m(ahead)
-                        round_means(ahead)
-                    if turns_next:
-                        turn(ahead + 1, 0)
-                    if prepares:
-                        quantise_means(ahead)
-                    if multiplies:
-                        mix_bank(here, 2)
-                    if prepares:
-                        quantise_a(ahead)
-                    if multiplies:
-                        add_out(here, 2)
-                    if finishes:
-                        activate(behind, 3)
-                    if turns_next:
-                        turn(ahead + 1, 1)
-                        pool(ahead + 1, 0)
-                    if prepares:
-                        quantise_sum_over_m(ahead)
-                    if multiplies:
-                        mix_bank(here, LAST)
+            turn(0, 0)
+            turn(0, 1)
+            pool(0, 0)
+            for i in range(-1, N_PIECES):
+                ahead, here, behind = i + 1, i, i - 1
+                prepares = ahead < N_PIECES
+                turns_next = ahead + 1 < N_PIECES
+                multiplies = 0 <= here < N_PIECES
+                finishes = 0 <= behind < N_PIECES
+                if 3 <= ahead + 2 < N_PIECES:
+                    tiles["raw", ahead + 2] = load(ahead + 2)
+                if finishes:
+                    add_out(behind, LAST)
+                if prepares:
+                    scale_a5(ahead)
+                    regroup_a_scalar(ahead)
+                if prepares:
+                    turn(ahead, 2)
+                    pool(ahead, 1)
+                if multiplies:
+                    terms_without_r(here)
+                if prepares:
+                    regroup_a_vector(ahead)
+                if multiplies:
+                    mix_bank(here, 0)
+                    add_out(here, 0)
+                if finishes:
+                    activate(behind, 0)
+                if prepares:
+                    turn(ahead, 3)
+                    pool(ahead, 2)
+                    sum_pairs_of_m(ahead)
+                if multiplies:
+                    mix_bank(here, 1)
+                    add_out(here, 1)
+                if finishes:
+                    activate(behind, 1)
+                    activate(behind, 2)
+                if prepares:
+                    pool(ahead, 3)
+                    finish_sum_over_m(ahead)
+                    round_means(ahead)
+                if turns_next:
+                    turn(ahead + 1, 0)
+                if prepares:
+                    quantise_means(ahead)
+                if multiplies:
+                    mix_bank(here, 2)
+                if prepares:
+                    quantise_a(ahead)
+                if multiplies:
+                    add_out(here, 2)
+                if finishes:
+                    activate(behind, 3)
+                if turns_next:
+                    turn(ahead + 1, 1)
+                    pool(ahead + 1, 0)
+                if prepares:
+                    quantise_sum_over_m(ahead)
+                if multiplies:
+                    mix_bank(here, LAST)
 
-        count = float(B * POSITIONS)
-        mean = keep.tile([P, O_TILES], F32)
-        nc.vector.tensor_reduce(out=mean[:], in_=sums[:], axis=AXIS_X, op=ALU.add)
-        nc.vector.tensor_scalar_mul(out=mean[:], in0=mean[:], scalar1=1.0 / count)
-        var = keep.tile([P, O_TILES], F32)
-        nc.vector.tensor_reduce(out=var[:], in_=squares[:], axis=AXIS_X, op=ALU.add)
-        nc.vector.tensor_scalar_mul(out=var[:], in0=var[:], scalar1=1.0 / count)
-        mean_sq = keep.tile([P, O_TILES], F32)
-        nc.vector.tensor_mul(out=mean_sq[:], in0=mean[:], in1=mean[:])
-        nc.vector.tensor_sub(out=var[:], in0=var[:], in1=mean_sq[:])
-        nc.vector.tensor_scalar(
-            out=var[:], in0=var[:], scalar1=0.0, scalar2=BN_EPS * UP * UP, op0=ALU.max, op1=ALU.add
-        )
-        std = keep.tile([P, O_TILES], F32)
-        nc.scalar.sqrt(out=std[:], in_=var[:])
-        gain = keep.tile([P, O_TILES], F32)
-        nc.vector.reciprocal(out=gain[:], in_=std[:])
-        nc.vector.tensor_mul(out=gain[:], in0=gain[:], in1=gamma_beta[:, 0:O_TILES])
-        shift = keep.tile([P, O_TILES], F32)
-        nc.vector.tensor_mul(out=shift[:], in0=mean[:], in1=gain[:])
-        nc.vector.tensor_sub(out=shift[:], in0=gamma_beta[:, O_TILES : 2 * O_TILES], in1=shift[:])
+            count = float(B * POSITIONS)
+            total = keep.tile([P, O_TILES], F32)
+            total_sq = keep.tile([P, O_TILES], F32)
+            mean_sq = keep.tile([P, O_TILES], F32)
+            var = keep.tile([P, O_TILES], F32)
+            std = keep.tile([P, O_TILES], F32)
+            gain = keep.tile([P, O_TILES], F32)
+            shift = keep.tile([P, O_TILES], F32)
+
+            def variance(ot):
+                col = slice(ot, ot + 1)
+                nc.vector.tensor_reduce(out=total[:, col], in_=sums[:, ot, :], axis=AXIS_X, op=ALU.add)
+                nc.vector.tensor_reduce(out=total_sq[:, col], in_=squares[:, ot, :], axis=AXIS_X, op=ALU.add)
+                nc.vector.scalar_tensor_tensor(
+                    out=mean_sq[:, col], in0=total[:, col], scalar=1.0 / (count * count), in1=total[:, col],
+                    op0=ALU.mult, op1=ALU.mult,
+                )
+                nc.vector.scalar_tensor_tensor(
+                    out=var[:, col], in0=total_sq[:, col], scalar=1.0 / count, in1=mean_sq[:, col],
+                    op0=ALU.mult, op1=ALU.subtract,
+                )
+                nc.vector.tensor_scalar(
+                    out=var[:, col], in0=var[:, col], scalar1=0.0, scalar2=BN_EPS * UP * UP,
+                    op0=ALU.max, op1=ALU.add,
+                )
+
+            def gain_and_shift(ot):
+                col = slice(ot, ot + 1)
+                nc.vector.reciprocal(out=gain[:, col], in_=std[:, col])
+                nc.vector.tensor_mul(out=gain[:, col], in0=gain[:, col], in1=gamma_beta[:, col])
+                nc.vector.scalar_tensor_tensor(
+                    out=shift[:, col], in0=total[:, col], scalar=1.0 / count, in1=gain[:, col],
+                    op0=ALU.mult, op1=ALU.mult,
+                )
+                nc.vector.tensor_sub(
+                    out=shift[:, col], in0=gamma_beta[:, O_TILES + ot : O_TILES + ot + 1], in1=shift[:, col]
+                )
+
+            def normalise(ot, step, staged):
+                b, m = divmod(step, M)
+                source = y[
+                    :, ot, b * PIECES_PER_B : (b + 1) * PIECES_PER_B, m * RUN : (m + 1) * RUN
+                ].rearrange("p q (th tl x) -> p th q x tl", tl=T_RUN, x=KR)
+                target = staged[:].rearrange("p q x (th tl) -> p th q x tl", tl=T_RUN)
+                for th in range(NT // T_RUN):
+                    if step % 2 == 0:
+                        nc.vector.tensor_scalar(
+                            out=target[:, th], in0=source[:, th], scalar1=gain[:, ot : ot + 1],
+                            scalar2=shift[:, ot : ot + 1], op0=ALU.mult, op1=ALU.add,
+                        )
+                    else:
+                        nc.scalar.activation(
+                            out=target[:, th], in_=source[:, th], func=ACT.Identity,
+                            bias=shift[:, ot : ot + 1], scale=gain[:, ot : ot + 1],
+                        )
+                nc.sync.dma_start(
+                    out=out[b].rearrange("(ot o) m k r t -> o ot m (k r t)", o=P)[:, ot, m, :],
+                    in_=staged[:].rearrange("p q x t -> p (q x t)"),
+                )
+
+            def stage_in_raw_buffer():
+                return raw_pool.tile([P, PIECES_PER_B, KR, NT], F32, name="raw")
+
+            final = N_PIECES - 1
+            activate(final, 0)
+            activate(final, 1)
+            variance(0)
+            nc.scalar.sqrt(out=std[:, 0:1], in_=var[:, 0:1])
+            add_out(final, LAST)
+            activate(final, 2)
+            activate(final, 3)
+            gain_and_shift(0)
+            normalise(0, 0, stage_in_raw_buffer())
+            variance(1)
+            normalise(0, 1, stage_in_raw_buffer())
+            nc.scalar.sqrt(out=std[:, 1:2], in_=var[:, 1:2])
+            normalise(0, 2, stage_in_raw_buffer())
+            gain_and_shift(1)
+            for step in range(3, B * M):
+                normalise(0, step, stage_in_raw_buffer())
 
         staged_pool = ctx.enter_context(tc.tile_pool(name="staged_pool", bufs=4))
-        step = 0
-        for b in range(B):
-            out_b = out[b].rearrange("(ot o) m k r t -> o ot m (k r t)", o=P)
-            for ot in range(O_TILES):
-                for m in range(M):
-                    source = y[
-                        :, ot, b * PIECES_PER_B : (b + 1) * PIECES_PER_B, m * RUN : (m + 1) * RUN
-                    ].rearrange("p q (th tl x) -> p th q x tl", tl=T_RUN, x=KR)
-                    staged = staged_pool.tile([P, PIECES_PER_B, KR, NT], F32)
-                    target = staged[:].rearrange("p q x (th tl) -> p th q x tl", tl=T_RUN)
-                    for th in range(NT // T_RUN):
-                        if step % 2 == 0:
-                            nc.vector.tensor_scalar(
-                                out=target[:, th], in0=source[:, th], scalar1=gain[:, ot : ot + 1],
-                                scalar2=shift[:, ot : ot + 1], op0=ALU.mult, op1=ALU.add,
-                            )
-                        else:
-                            nc.scalar.activation(
-                                out=target[:, th], in_=source[:, th], func=ACT.Identity,
-                                bias=shift[:, ot : ot + 1], scale=gain[:, ot : ot + 1],
-                            )
-                    nc.sync.dma_start(
-                        out=out_b[:, ot, m, :], in_=staged[:].rearrange("p q x t -> p (q x t)")
-                    )
-                    step += 1
+        for step in range(B * M):
+            staged = staged_pool.tile([P, PIECES_PER_B, KR, NT], F32)
+            normalise(1, step, staged)

@@ -269,16 +269,20 @@ def tile_layer_3d_dep_pa_t_kernel(tc, A, P1, P2, P3, P4, a5, gamma, beta, out):
                         .unsqueeze(1)
                         .to_broadcast([P, NT, KR]),
                     )
+                tiles["small_codes", piece] = small_codes
+                tiles["at_rep_codes", piece], tiles["at_rep_scales", piece] = at_rep_codes, at_rep_scales
+
+            def repeat_scales(piece):
                 nc.vector.tensor_copy(
-                    out=at_rep_scales[:].bitcast(I32).rearrange("p (m t x) -> p m t x", m=M, t=NT),
-                    in_=scales[:, 0:SMALL]
+                    out=tiles["at_rep_scales", piece][:]
+                    .bitcast(I32)
+                    .rearrange("p (m t x) -> p m t x", m=M, t=NT),
+                    in_=small_scales[piece % 2][:, 0:SMALL]
                     .bitcast(I32)
                     .rearrange("p (m x) -> p m x", m=M)
                     .unsqueeze(2)
                     .to_broadcast([P, M, NT, KR // 4]),
                 )
-                tiles["small_codes", piece] = small_codes
-                tiles["at_rep_codes", piece], tiles["at_rep_scales", piece] = at_rep_codes, at_rep_scales
 
             def quantise_sum_over_m(piece):
                 nc.vector.quantize_mx(
@@ -419,19 +423,17 @@ def tile_layer_3d_dep_pa_t_kernel(tc, A, P1, P2, P3, P4, a5, gamma, beta, out):
                     turn(ahead + 1, 0)
                 if prepares:
                     quantise_means(ahead)
+                    quantise_a(ahead)
+                    quantise_sum_over_m(ahead)
+                    repeat_scales(ahead)
                 if multiplies:
                     mix_bank(here, 2)
-                if prepares:
-                    quantise_a(ahead)
-                if multiplies:
                     add_out(here, 2)
                 if finishes:
                     activate(behind, 3)
                 if turns_next:
                     turn(ahead + 1, 1)
                     pool(ahead + 1, 0)
-                if prepares:
-                    quantise_sum_over_m(ahead)
                 if multiplies:
                     mix_bank(here, LAST)
 

from contextlib import ExitStack

import concourse.mybir as mybir
from concourse.masks import make_identity

BF16 = mybir.dt.bfloat16
F32 = mybir.dt.float32
I32 = mybir.dt.int32
U32 = mybir.dt.uint32
U8 = mybir.dt.uint8
FP8X4 = mybir.dt.float8_e4m3fn_x4
ALU = mybir.AluOpType
ACT = mybir.ActivationFunctionType
AXIS_X = mybir.AxisListType.X

B, C, O, M, K, NR, NT = 2, 512, 256, 4, 32, 8, 8
BN_EPS = 1e-5
P = 128
PACK = 4
O_TILES = O // P
POSITIONS = M * K * NR * NT

K_PIECE = 4
PIECES_PER_B = K // K_PIECE
N_PIECES = B * PIECES_PER_B
KR = K_PIECE * NR
RUN = K_PIECE * NR * NT
COLS = M * RUN
SMALL = M * KR
HALVES = RUN // P
K_SQUARE = K_PIECE // HALVES
T_RUN = NT // 2
POOLED = K_SQUARE * NR
SMALL_COLS = 2 * SMALL + RUN

UP = 10.0
STATIONARY = (("p1", 8.0), ("p1", 2.0), ("p2", 1.0 / M), ("p3", 1.0), ("p4", 1.0))
W_A1_HI, W_A1_LO, W_A2, W_A3, W_A4 = 0, 1, 2, 3, 4

FLOPS = 2 * O * C * B * POSITIONS * (8 + 2 + 1 + 1) // 8


def tile_layer_3d_dep_pa_t_kernel(tc, A, P1, P2, P3, P4, a5, gamma, beta, out):
    nc = tc.nc
    weights = {"p1": P1, "p2": P2, "p3": P3, "p4": P4}

    with ExitStack() as ctx:
        keep = ctx.enter_context(tc.tile_pool(name="keep", bufs=1))
        psum_x = ctx.enter_context(tc.psum_pool(name="psum_x", bufs=3))
        psum_turned = ctx.enter_context(tc.psum_pool(name="psum_turned", bufs=2))
        psum_pooled = ctx.enter_context(tc.psum_pool(name="psum_pooled", bufs=2))
        psum_small = ctx.enter_context(tc.psum_pool(name="psum_small", bufs=1))

        w_codes = keep.tile([P, len(STATIONARY), O], U32, align_bytes=64)
        w_scales = keep.tile([P, len(STATIONARY), O], U8, align_bytes=64)
        a5_sb = keep.tile([P, B * O_TILES, M * K * NT], BF16)
        gamma_beta = keep.tile([P, 2 * O_TILES], F32)
        y = keep.tile([P, O_TILES, N_PIECES, COLS], F32)
        sums = keep.tile([P, O_TILES, N_PIECES], F32)
        squares = keep.tile([P, O_TILES, N_PIECES], F32)
        small_scales = [
            keep.tile([P, SMALL_COLS], U8, align_bytes=64, name="small_scales%d" % parity)
            for parity in range(2)
        ]
        for parity in range(2):
            nc.vector.memset(small_scales[parity][:].bitcast(I32), 0)
        ident_bf16 = keep.tile([P, P], BF16)
        make_identity(nc, ident_bf16[:])
        pool_mat = keep.tile([P, 2, POOLED], BF16)

        table_warmer = keep.tile([P, 1], F32)
        nc.vector.memset(table_warmer[:], 1.0)
        nc.scalar.sqrt(out=table_warmer[:], in_=table_warmer[:])

        raw_pool = ctx.enter_context(tc.tile_pool(name="raw_pool", bufs=3))

        def load(piece):
            b, kq = divmod(piece, PIECES_PER_B)
            raw = raw_pool.tile([P, PACK, M, RUN], BF16, name="raw")
            nc.sync.dma_start(
                out=raw[:],
                in_=A[b].rearrange("(p j) m k r t -> p j m (k r t)", j=PACK)[
                    :, :, :, kq * RUN : (kq + 1) * RUN
                ],
            )
            return raw

        ctx.enter_context(tc.manual_schedule())

        with tc.tile_pool(name="setup", bufs=2) as setup:
            gb_rows = setup.tile([P, P], BF16, tag="gb_rows")
            nc.vector.memset(gb_rows[:], 0.0)
            ident_f32 = setup.tile([P, P], F32, tag="ident_f32")
            make_identity(nc, ident_f32[:])

            pool_ones = setup.tile([P, 2, POOLED], F32, tag="pool_ones")
            nc.vector.tensor_reduce(
                out=pool_ones[:, 0, :],
                in_=ident_f32[:].rearrange("p (x t) -> p x t", t=NT),
                axis=AXIS_X,
                op=ALU.add,
            )
            nc.vector.tensor_reduce(
                out=pool_ones[:, 1, :].rearrange("p (k t) -> p k t", t=NT),
                in_=ident_f32[:].rearrange("p (k r t) -> p k t r", r=NR, t=NT),
                axis=AXIS_X,
                op=ALU.add,
            )
            nc.vector.tensor_scalar_mul(out=pool_mat[:, 0, :], in0=pool_ones[:, 0, :], scalar1=1.0 / NT)
            nc.vector.tensor_scalar_mul(out=pool_mat[:, 1, :], in0=pool_ones[:, 1, :], scalar1=1.0 / NR)

            all_w_rows = {}
            for name in ("p1", "p2", "p3", "p4"):
                w_rows = setup.tile([P, O_TILES, C], BF16, name="w_rows_" + name, bufs=1)
                nc.sync.dma_start(
                    out=w_rows[:], in_=weights[name].rearrange("(ot o) c -> o ot c", o=P)
                )
                all_w_rows[name] = w_rows
            nc.sync.dma_start(out=gb_rows[0:O_TILES, :], in_=gamma.rearrange("(ot o) -> ot o", o=P))
            nc.sync.dma_start(
                out=gb_rows[O_TILES : 2 * O_TILES, :], in_=beta.rearrange("(ot o) -> ot o", o=P)
            )
            first_raws = {0: load(0), 1: load(1)}
            nc.sync.dma_start(
                out=a5_sb[:], in_=a5.rearrange("b (ot o) m k t -> o (b ot) (m k t)", o=P)
            )
            first_raws[2] = load(2)

            grouped_w = {}
            for name in ("p1", "p2", "p3", "p4"):
                w_rows = all_w_rows[name]
                words = w_rows[:].bitcast(F32).rearrange("o ot (p u) -> o ot u p", u=2)
                turned = psum_x.tile([P, O_TILES, 2, P], F32, name="acc")
                for ot in range(O_TILES):
                    for u in range(2):
                        nc.tensor.transpose(turned[:, ot, u, :], words[:, ot, u, :], ident_f32[:])
                grouped = setup.tile([P, O * PACK], BF16, name="grouped_" + name, bufs=1, align_bytes=64)
                nc.scalar.copy(
                    out=grouped[:].bitcast(F32).rearrange("p (ot o u) -> p ot o u", ot=O_TILES, u=2),
                    in_=turned[:].rearrange("p ot u o -> p ot o u"),
                )
                grouped_w[name] = grouped

            for i, (name, factor) in enumerate(STATIONARY):
                scaled = grouped_w[name]
                if factor != 1.0:
                    scaled = setup.tile([P, O * PACK], BF16, tag="scaled", align_bytes=64)
                    nc.vector.tensor_scalar_mul(out=scaled[:], in0=grouped_w[name][:], scalar1=factor)
                nc.vector.quantize_mx(
                    out=w_codes[:, i, :].bitcast(FP8X4), scales=w_scales[:, i, :], in_=scaled[:]
                )

            gb_turned = psum_small.tile([P, P], BF16, tag="small")
            nc.tensor.transpose(gb_turned[:], gb_rows[:], ident_bf16[:])
            nc.vector.tensor_copy(out=gamma_beta[:], in_=gb_turned[:, 0 : 2 * O_TILES])

        with tc.tile_pool(name="once", bufs=1) as once, tc.tile_pool(name="twice", bufs=2) as twice:

            def mix(acc, weight, ot, codes, scales, start, stop):
                nc.tensor.matmul_mx(
                    out=acc,
                    lhsT=w_codes[:, weight, ot * P : (ot + 1) * P].bitcast(FP8X4),
                    lhsT_scale=w_scales[:, weight, ot * P : (ot + 1) * P],
                    rhs=codes.bitcast(FP8X4),
                    rhs_scale=scales,
                    start=start,
                    stop=stop,
                )

            tiles = {("raw", piece): first_raws[piece] for piece in first_raws}

            def regroup_a_scalar(piece):
                raw = tiles["raw", piece]
                grouped_a = once.tile([P, COLS, PACK], BF16, align_bytes=64, name="grouped_a")
                target = grouped_a[:].rearrange("p (m th tl x) j -> p th m x j tl", m=M, tl=T_RUN, x=KR)
                source = raw[:].rearrange("p j m (x th tl) -> p th m x j tl", x=KR, tl=T_RUN)
                for m in range(M // 2, M):
                    nc.scalar.copy(out=target[:, 1, m], in_=source[:, 1, m])
                tiles["grouped_a", piece] = grouped_a
                tiles["regroup_views", piece] = (target, source)

            def regroup_a_vector(piece):
                target, source = tiles["regroup_views", piece]
                nc.vector.tensor_copy(out=target[:, 0], in_=source[:, 0])
                nc.vector.tensor_copy(out=target[:, 1, 0 : M // 2], in_=source[:, 1, 0 : M // 2])

            def sum_pairs_of_m(piece):
                by_m = tiles["grouped_a", piece][:].rearrange("p (m w) j -> p m (w j)", m=M)
                pair_sums = once.tile([P, 2, RUN * PACK], F32, name="pair_sums")
                nc.vector.tensor_add(out=pair_sums[:], in0=by_m[:, 0:2, :], in1=by_m[:, 2:4, :])
                tiles["pair_sums", piece] = pair_sums

            def quantise_a(piece):
                a_codes = twice.tile([P, COLS], U32, align_bytes=64, name="a_codes")
                a_scales = twice.tile([P, COLS], U8, align_bytes=64, name="a_scales")
                nc.vector.quantize_mx(
                    out=a_codes[:].bitcast(FP8X4),
                    scales=a_scales[:],
                    in_=tiles["grouped_a", piece][:].rearrange("p w j -> p (w j)"),
                )
                tiles["a_codes", piece], tiles["a_scales", piece] = a_codes, a_scales

            def finish_sum_over_m(piece):
                pair_sums = tiles["pair_sums", piece]
                grouped_small = once.tile([P, SMALL_COLS * PACK], BF16, align_bytes=64, name="grouped_small")
                nc.vector.tensor_add(
                    out=grouped_small[:, 2 * SMALL * PACK :], in0=pair_sums[:, 0, :], in1=pair_sums[:, 1, :]
                )
                tiles["grouped_small", piece] = grouped_small

            def turn(piece, j):
                raw = tiles["raw", piece]
                turned_ps = psum_turned.tile([P, M, HALVES, P], BF16, name="turned_ps")
                for m in range(M):
                    for h in range(HALVES):
                        nc.tensor.transpose(
                            turned_ps[:, m, h, :], raw[:, j, m, h * P : (h + 1) * P], ident_bf16[:]
                        )
                turned = twice.tile([P, M, HALVES, P], BF16, name="turned")
                nc.scalar.copy(
                    out=turned[:].rearrange("p m h c -> p (m h c)").bitcast(F32),
                    in_=turned_ps[:].rearrange("p m h c -> p (m h c)").bitcast(F32),
                )
                tiles["turned", piece, j] = turned

            def pool(piece, j):
                if j == 0:
                    for i in range(M // 2):
                        tiles["pooled", piece, i] = psum_pooled.tile(
                            [P, 2, PACK, 2, HALVES, POOLED], F32, name="pooled%d" % i, tag="pooled"
                        )
                for m in range(M):
                    for h in range(HALVES):
                        nc.tensor.matmul(
                            out=tiles["pooled", piece, m // 2][:, :, j, m % 2, h, :],
                            lhsT=tiles["turned", piece, j][:, m, h, :],
                            rhs=pool_mat[:],
                            start=True,
                            stop=True,
                        )

            def round_means(piece):
                grouped_tr = tiles["grouped_small", piece][:, 0 : 2 * SMALL * PACK].rearrange(
                    "p (s w j) -> p s w j", s=2, j=PACK
                )
                for i in range(M // 2):
                    nc.scalar.copy(
                        out=grouped_tr[:, :, i * (SMALL // 2) : (i + 1) * (SMALL // 2), :],
                        in_=tiles["pooled", piece, i][:].rearrange("p s j m h x -> p s (m h x) j"),
                    )

            def quantise_means(piece):
                small_codes = twice.tile([P, SMALL_COLS], U32, align_bytes=64, name="small_codes")
                scales = small_scales[piece % 2]
                nc.vector.quantize_mx(
                    out=small_codes[:, 0 : 2 * SMALL].bitcast(FP8X4),
                    scales=scales[:, 0 : 2 * SMALL],
                    in_=tiles["grouped_small", piece][:, 0 : 2 * SMALL * PACK],
                )
                at_rep_codes = twice.tile([P, COLS], U32, align_bytes=64, name="at_rep_codes")
                at_rep_scales = twice.tile([P, COLS], U8, align_bytes=64, name="at_rep_scales")
                for m in range(M):
                    nc.sync.dma_start(
                        out=at_rep_codes[:, m * RUN : (m + 1) * RUN]
                        .bitcast(I32)
                        .rearrange("p (t x) -> p t x", t=NT),
                        in_=small_codes[:, m * KR : (m + 1) * KR]
                        .bitcast(I32)
                        .unsqueeze(1)
                        .to_broadcast([P, NT, KR]),
                    )
                tiles["small_codes", piece] = small_codes
                tiles["at_rep_codes", piece], tiles["at_rep_scales", piece] = at_rep_codes, at_rep_scales

            def repeat_scales(piece):
                nc.vector.tensor_copy(
                    out=tiles["at_rep_scales", piece][:]
                    .bitcast(I32)
                    .rearrange("p (m t x) -> p m t x", m=M, t=NT),
                    in_=small_scales[piece % 2][:, 0:SMALL]
                    .bitcast(I32)
                    .rearrange("p (m x) -> p m x", m=M)
                    .unsqueeze(2)
                    .to_broadcast([P, M, NT, KR // 4]),
                )

            def quantise_sum_over_m(piece):
                nc.vector.quantize_mx(
                    out=tiles["small_codes", piece][:, 2 * SMALL :].bitcast(FP8X4),
                    scales=small_scales[piece % 2][:, 2 * SMALL :],
                    in_=tiles["grouped_small", piece][:, 2 * SMALL * PACK :],
                )

            def scale_a5(piece):
                b, kq = divmod(piece, PIECES_PER_B)
                a5_of_b = a5_sb[:].rearrange("p g x -> p (g x)")[
                    :, b * O_TILES * M * K * NT : (b + 1) * O_TILES * M * K * NT
                ]
                a5_scaled = twice.tile([P, O_TILES * M, NT * K_PIECE], F32, name="a5_scaled")
                nc.gpsimd.tensor_scalar(
                    out=a5_scaled[:].rearrange("p g (t k) -> p g t k", t=NT),
                    in0=a5_of_b.rearrange(
                        "p (g kq k t) -> p kq g t k", kq=PIECES_PER_B, k=K_PIECE, t=NT
                    )[:, kq],
                    scalar1=2.0 / 0.5,
                    scalar2=0.0,
                    op0=ALU.mult,
                    op1=ALU.add,
                )
                tiles["a5_scaled", piece] = a5_scaled

            def terms_without_r(piece):
                ar_codes = tiles["small_codes", piece][:, SMALL : 2 * SMALL]
                ar_scales = small_scales[piece % 2][:, SMALL : 2 * SMALL]
                a4_acc = psum_small.tile([P, O_TILES * SMALL], F32, tag="small", name="a4_acc")
                for ot in range(O_TILES):
                    a4_cols = a4_acc[:, ot * SMALL : (ot + 1) * SMALL]
                    mix(a4_cols, W_A4, ot, ar_codes, ar_scales, True, True)
                no_r = twice.tile([P, O_TILES * M, NT * K_PIECE], F32, name="no_r")
                nc.vector.tensor_tensor(
                    out=no_r[:].rearrange("p g (t k) -> p g t k", t=NT),
                    in0=a4_acc[:].rearrange("p (g k t) -> p g t k", k=K_PIECE, t=NT),
                    in1=tiles["a5_scaled", piece][:].rearrange("p g (t k) -> p g t k", t=NT),
                    op=ALU.add,
                )
                tiles["no_r", piece] = no_r

            def mix_bank(piece, bank):
                ot, m_pair = divmod(bank, M // 2)
                acc = psum_x.tile([P, 2, RUN], F32, name="acc")
                am_codes = tiles["small_codes", piece][:, 2 * SMALL :]
                am_scales = small_scales[piece % 2][:, 2 * SMALL :]
                for i in range(2):
                    cols = slice((2 * m_pair + i) * RUN, (2 * m_pair + i + 1) * RUN)
                    a_codes, a_scales = tiles["a_codes", piece][:, cols], tiles["a_scales", piece][:, cols]
                    mix(acc[:, i, :], W_A1_HI, ot, a_codes, a_scales, True, False)
                    mix(acc[:, i, :], W_A1_LO, ot, a_codes, a_scales, False, False)
                    mix(acc[:, i, :], W_A2, ot, am_codes, am_scales, False, False)
                    mix(
                        acc[:, i, :], W_A3, ot, tiles["at_rep_codes", piece][:, cols],
                        tiles["at_rep_scales", piece][:, cols], False, True,
                    )
                tiles["acc", piece, bank] = acc

            def add_out(piece, bank):
                ot, m_pair = divmod(bank, M // 2)
                acc = tiles["acc", piece, bank]
                g = ot * M + 2 * m_pair
                nc.vector.scalar_tensor_tensor(
                    out=y[:, ot, piece, 2 * m_pair * RUN : (2 * m_pair + 2) * RUN].rearrange(
                        "p (x r) -> p x r", r=NR
                    ),
                    in0=tiles["no_r", piece][:, g : g + 2, :]
                    .rearrange("p g x -> p (g x)")
                    .unsqueeze(2)
                    .to_broadcast([P, 2 * NT * K_PIECE, NR]),
                    scalar=0.5 * UP,
                    in1=acc[:].rearrange("p i (x r) -> p (i x) r", r=NR),
                    op0=ALU.mult,
                    op1=ALU.add,
                )

            def activate(piece, part):
                ot, second = divmod(part, 2)
                y_piece = y[:, ot, piece, :]
                if not second:
                    nc.scalar.activation(
                        out=y_piece, in_=y_piece, func=ACT.Relu,
                        accum_out=sums[:, ot, piece : piece + 1],
                    )
                else:
                    squared = twice.tile([P, COLS], BF16, name="squared")
                    nc.scalar.activation(
                        out=squared[:], in_=y_piece, func=ACT.Square,
                        accum_out=squares[:, ot, piece : piece + 1],
                    )

            assert PACK == O_TILES * (M // 2)
            LAST = PACK - 1
            turn(0, 0)
            turn(0, 1)
            pool(0, 0)
            for i in range(-1, N_PIECES):
                ahead, here, behind = i + 1, i, i - 1
                prepares = ahead < N_PIECES
                turns_next = ahead + 1 < N_PIECES
                multiplies = 0 <= here < N_PIECES
                finishes = 0 <= behind < N_PIECES
                if 3 <= ahead + 2 < N_PIECES:
                    tiles["raw", ahead + 2] = load(ahead + 2)
                if finishes:
                    add_out(behind, LAST)
                if prepares:
                    scale_a5(ahead)
                    regroup_a_scalar(ahead)
                if prepares:
                    turn(ahead, 2)
                    pool(ahead, 1)
                if multiplies:
                    terms_without_r(here)
                if prepares:
                    regroup_a_vector(ahead)
                if multiplies:
                    mix_bank(here, 0)
                    add_out(here, 0)
                if finishes:
                    activate(behind, 0)
                if prepares:
                    turn(ahead, 3)
                    pool(ahead, 2)
                    sum_pairs_of_m(ahead)
                if multiplies:
                    mix_bank(here, 1)
                    add_out(here, 1)
                if finishes:
                    activate(behind, 1)
                    activate(behind, 2)
                if prepares:
                    pool(ahead, 3)
                    finish_sum_over_m(ahead)
                    round_means(ahead)
                if turns_next:
                    turn(ahead + 1, 0)
                if prepares:
                    quantise_means(ahead)
                    quantise_a(ahead)
                    quantise_sum_over_m(ahead)
                    repeat_scales(ahead)
                if multiplies:
                    mix_bank(here, 2)
                    add_out(here, 2)
                if finishes:
                    activate(behind, 3)
                if turns_next:
                    turn(ahead + 1, 1)
                    pool(ahead + 1, 0)
                if multiplies:
                    mix_bank(here, LAST)

            count = float(B * POSITIONS)
            total = keep.tile([P, O_TILES], F32)
            total_sq = keep.tile([P, O_TILES], F32)
            mean_sq = keep.tile([P, O_TILES], F32)
            var = keep.tile([P, O_TILES], F32)
            std = keep.tile([P, O_TILES], F32)
            gain = keep.tile([P, O_TILES], F32)
            shift = keep.tile([P, O_TILES], F32)

            def variance(ot):
                col = slice(ot, ot + 1)
                nc.vector.tensor_reduce(out=total[:, col], in_=sums[:, ot, :], axis=AXIS_X, op=ALU.add)
                nc.vector.tensor_reduce(out=total_sq[:, col], in_=squares[:, ot, :], axis=AXIS_X, op=ALU.add)
                nc.vector.scalar_tensor_tensor(
                    out=mean_sq[:, col], in0=total[:, col], scalar=1.0 / (count * count), in1=total[:, col],
                    op0=ALU.mult, op1=ALU.mult,
                )
                nc.vector.scalar_tensor_tensor(
                    out=var[:, col], in0=total_sq[:, col], scalar=1.0 / count, in1=mean_sq[:, col],
                    op0=ALU.mult, op1=ALU.subtract,
                )
                nc.vector.tensor_scalar(
                    out=var[:, col], in0=var[:, col], scalar1=0.0, scalar2=BN_EPS * UP * UP,
                    op0=ALU.max, op1=ALU.add,
                )

            def gain_and_shift(ot):
                col = slice(ot, ot + 1)
                nc.vector.reciprocal(out=gain[:, col], in_=std[:, col])
                nc.vector.tensor_mul(out=gain[:, col], in0=gain[:, col], in1=gamma_beta[:, col])
                nc.vector.scalar_tensor_tensor(
                    out=shift[:, col], in0=total[:, col], scalar=1.0 / count, in1=gain[:, col],
                    op0=ALU.mult, op1=ALU.mult,
                )
                nc.vector.tensor_sub(
                    out=shift[:, col], in0=gamma_beta[:, O_TILES + ot : O_TILES + ot + 1], in1=shift[:, col]
                )

            def normalise(ot, step, staged):
                b, m = divmod(step, M)
                source = y[
                    :, ot, b * PIECES_PER_B : (b + 1) * PIECES_PER_B, m * RUN : (m + 1) * RUN
                ].rearrange("p q (th tl x) -> p th q x tl", tl=T_RUN, x=KR)
                target = staged[:].rearrange("p q x (th tl) -> p th q x tl", tl=T_RUN)
                for th in range(NT // T_RUN):
                    if step % 2 == 0:
                        nc.vector.tensor_scalar(
                            out=target[:, th], in0=source[:, th], scalar1=gain[:, ot : ot + 1],
                            scalar2=shift[:, ot : ot + 1], op0=ALU.mult, op1=ALU.add,
                        )
                    else:
                        nc.scalar.activation(
                            out=target[:, th], in_=source[:, th], func=ACT.Identity,
                            bias=shift[:, ot : ot + 1], scale=gain[:, ot : ot + 1],
                        )
                nc.sync.dma_start(
                    out=out[b].rearrange("(ot o) m k r t -> o ot m (k r t)", o=P)[:, ot, m, :],
                    in_=staged[:].rearrange("p q x t -> p (q x t)"),
                )

            def stage_in_raw_buffer():
                return raw_pool.tile([P, PIECES_PER_B, KR, NT], F32, name="raw")

            final = N_PIECES - 1
            activate(final, 0)
            activate(final, 1)
            variance(0)
            nc.scalar.sqrt(out=std[:, 0:1], in_=var[:, 0:1])
            add_out(final, LAST)
            activate(final, 2)
            activate(final, 3)
            gain_and_shift(0)
            normalise(0, 0, stage_in_raw_buffer())
            variance(1)
            normalise(0, 1, stage_in_raw_buffer())
            nc.scalar.sqrt(out=std[:, 1:2], in_=var[:, 1:2])
            normalise(0, 2, stage_in_raw_buffer())
            gain_and_shift(1)
            for step in range(3, B * M):
                normalise(0, step, stage_in_raw_buffer())

        staged_pool = ctx.enter_context(tc.tile_pool(name="staged_pool", bufs=4))
        for step in range(B * M):
            staged = staged_pool.tile([P, PIECES_PER_B, KR, NT], F32)
            normalise(1, step, staged)
